import numpy as np
import ml_dtypes


def mxq(x, axis, fmt="e4m3"):
    dtype, down = {"e4m3": (ml_dtypes.float8_e4m3fn, 7), "e5m2": (ml_dtypes.float8_e5m2, 14)}[fmt]
    v = np.moveaxis(np.asarray(x, np.float32).astype(ml_dtypes.bfloat16).astype(np.float64), axis, -1)
    blocks = v.reshape(v.shape[:-1] + (-1, 32))
    amax = np.abs(blocks).max(-1, keepdims=True)
    byte = np.maximum(np.where(amax > 0, np.frexp(amax)[1] - 1 + 127, 0) - down, 1)
    scale = np.exp2(byte - 127.0)
    codes = (blocks / scale).astype(np.float32).astype(dtype).astype(np.float64)
    return np.moveaxis((codes * scale).reshape(v.shape), -1, axis)


WIDE = False


def mx_kscale(k):
    if not WIDE:
        return np.ones(k)
    levels = np.array([10, -10, 5, -5, 0])
    a = np.random.permutation(np.resize(levels, k // 512 * 4)).reshape(k // 512, 4)
    idx = np.arange(k)
    return np.exp2(a[idx // 512, idx % 128 // 32])


BF16 = ml_dtypes.bfloat16


def bf(x):
    return np.asarray(x, np.float32).astype(BF16)


def f64(x):
    return np.asarray(x).astype(np.float64)


B, D_IN, D_OUT = 256, 2048, 2048


def sigmoid(v):
    return 1.0 / (1.0 + np.exp(-v))


def setup_inputs():
    s = mx_kscale(D_IN)
    w = lambda: bf(np.random.standard_normal((D_IN, D_OUT)) / np.sqrt(D_IN) / s[:, None])
    b = lambda: bf(np.random.standard_normal(D_OUT) * 0.5)
    return {"x": bf(np.random.standard_normal((B, D_IN)) * s),
            "Wxi": w(), "bxi": b(),
            "Wxc": w(), "bxc": b(),
            "Wxo": w(), "bxo": b()}


def reference(x, Wxi, bxi, Wxc, bxc, Wxo, bxo):
    xq = mxq(f64(x), 1, "e4m3")
    gi = (xq @ mxq(f64(Wxi), 0, "e4m3")) + f64(bxi)
    gc = (xq @ mxq(f64(Wxc), 0, "e4m3")) + f64(bxc)
    go = (xq @ mxq(f64(Wxo), 0, "e4m3")) + f64(bxo)
    i = sigmoid(gi)
    c = np.tanh(gc)
    o = sigmoid(go)
    new_state = c * i
    return np.tanh(new_state) * o

@@ -1,0 +1,274 @@
+from contextlib import ExitStack
+
+import concourse.mybir as mybir
+from concourse.masks import make_identity
+
+F32 = mybir.dt.float32
+BF16 = mybir.dt.bfloat16
+I32 = mybir.dt.int32
+U32 = mybir.dt.uint32
+U8 = mybir.dt.uint8
+FP8X4 = mybir.dt.float8_e4m3fn_x4
+ACT = mybir.ActivationFunctionType
+
+P = 128
+PACK = 4
+K_PASS = P * PACK
+
+B, D_IN, D_OUT = 256, 2048, 2048
+GATES = 3
+PASSES = D_IN // K_PASS
+M_TILES = B // P
+N_TILES = D_OUT // P
+SLICE = 512
+SLICES = D_OUT // SLICE
+SLICE_TILES = SLICE // P
+
+PLAIN_VECTOR_COLS = 240
+BUSY_VECTOR_COLS = 336
+
+RAW_BUFS = 4
+QUANTISE_LAG = 2
+PERIOD = 2
+
+FLOPS = 2 * B * D_IN * D_OUT * GATES
+
+
+def unit_order():
+    units = []
+    for g in range(GATES):
+        by_pass = PASSES if g < GATES - 1 else PASSES // 2
+        units.extend([(g, c, s) for c in range(by_pass) for s in range(SLICES)])
+        units.extend([(g, c, s) for s in range(SLICES) for c in range(by_pass, PASSES)])
+    return units
+
+
+def load_biases(nc, const, biases):
+    bias_rows = const.tile([P, P], BF16)
+    nc.vector.memset(bias_rows[:].bitcast(I32), 0)
+    for g in range(GATES):
+        nc.sync.dma_start(
+            out=bias_rows[g * N_TILES : (g + 1) * N_TILES, :],
+            in_=biases[g].rearrange("(t n) -> t n", n=P),
+        )
+    return bias_rows
+
+
+def turn_biases(nc, const, turn_psum, identity, bias_rows):
+    bias_rows_f32 = const.tile([P, P], F32)
+    nc.vector.tensor_copy(out=bias_rows_f32[:], in_=bias_rows[:])
+    bias_turned = turn_psum.tile([P, P], F32, tag="turned")
+    nc.tensor.transpose(bias_turned[:], bias_rows_f32[:], identity[:])
+    bias_cols = const.tile([P, P], F32)
+    nc.vector.tensor_copy(out=bias_cols[:], in_=bias_turned[:])
+    return bias_cols
+
+
+def quantise_x(nc, grouped_pool, turn_psum, identity, x_rows, x_codes, x_scales):
+    x_words = x_rows[:].bitcast(F32).rearrange(
+        "p (a c q u) -> p a c u q", a=M_TILES, c=PASSES, q=P, u=2
+    )
+    for c in range(PASSES):
+        turned = turn_psum.tile([P, 2, B], F32, tag="turned")
+        for u in range(2):
+            for a in range(M_TILES):
+                nc.tensor.transpose(
+                    turned[:, u, a * P : (a + 1) * P], x_words[:, a, c, u, :], identity[:]
+                )
+        x_grouped = grouped_pool.tile([P, B * PACK], BF16, tag="grouped", align_bytes=64)
+        nc.scalar.copy(
+            out=x_grouped[:].bitcast(F32).rearrange("p (m u) -> p m u", u=2),
+            in_=turned.rearrange("p u m -> p m u"),
+        )
+        nc.vector.quantize_mx(
+            out=x_codes[:, c, :].bitcast(FP8X4), scales=x_scales[:, c, :], in_=x_grouped[:]
+        )
+
+
+def regroup_slice(nc, grouped_pool, raw, s, vector_cols):
+    grouped = grouped_pool.tile([P, SLICE, PACK], BF16, tag="grouped", align_bytes=64)
+    first = s * SLICE
+    nc.vector.tensor_copy(
+        out=grouped[:, :vector_cols, :].rearrange("p (r i) j -> p r j i", i=4),
+        in_=raw[:, :, first : first + vector_cols].rearrange("p j (r i) -> p r j i", i=4),
+    )
+    nc.scalar.copy(
+        out=grouped[:, vector_cols:, :].rearrange("p (r i) j -> p r j i", i=4),
+        in_=raw[:, :, first + vector_cols : first + SLICE].rearrange(
+            "p j (r i) -> p r j i", i=4
+        ),
+    )
+    return grouped
+
+
+def turn_slice(nc, turn_psum, identity, values):
+    banks = []
+    for a in range(M_TILES):
+        bank = turn_psum.tile([P, SLICE], F32, tag="turned", name="bank")
+        for t in range(SLICE_TILES):
+            nc.tensor.transpose(
+                bank[:, t * P : (t + 1) * P], values[:, t, a * P : (a + 1) * P], identity[:]
+            )
+        banks.append(bank)
+    return banks
+
+
+def tile_lstm_pa_kernel(tc, x, Wxi, bxi, Wxc, bxc, Wxo, bxo, out):
+    nc = tc.nc
+    weights = [Wxi, Wxc, Wxo]
+    functions = [ACT.Sigmoid, ACT.Tanh, ACT.Sigmoid]
+    out_view = out.rearrange("(a p) n -> p a n", p=P)
+
+    with ExitStack() as ctx:
+        ctx.enter_context(tc.manual_schedule())
+        const = ctx.enter_context(tc.tile_pool(name="const", bufs=1))
+        raw_pool = ctx.enter_context(tc.tile_pool(name="raw", bufs=RAW_BUFS))
+        grouped_pool = ctx.enter_context(tc.tile_pool(name="grouped", bufs=4))
+        quantised = ctx.enter_context(tc.tile_pool(name="quantised", bufs=2))
+        work = ctx.enter_context(tc.tile_pool(name="work", bufs=2))
+        acc_psum = ctx.enter_context(tc.psum_pool(name="acc", bufs=4))
+        turn_psum = ctx.enter_context(tc.psum_pool(name="turn", bufs=4))
+
+        identity = const.tile([P, P], F32)
+        make_identity(nc, identity[:])
+        x_rows = const.tile([P, M_TILES * D_IN], BF16)
+        x_codes = const.tile([P, PASSES, B], U32, align_bytes=64)
+        x_scales = const.tile([P, PASSES, B], U8, align_bytes=64)
+        i_gate = const.tile([P, N_TILES, B], F32)
+        tanh_state = const.tile([P, M_TILES, D_OUT], F32)
+
+        raws = {}
+        codes = {}
+        accs = {}
+        gates = {}
+        turned_banks = {}
+
+        def load_pass(k):
+            g, c = divmod(k, PASSES)
+            raw = raw_pool.tile([P, PACK, D_OUT], BF16, tag="raw")
+            nc.sync.dma_start(
+                out=raw[:],
+                in_=weights[g][c * K_PASS : (c + 1) * K_PASS, :].rearrange(
+                    "(p j) w -> p j w", j=PACK
+                ),
+            )
+            raws[(g, c)] = raw
+
+        def quantise_unit(grouped, g, c, s):
+            w_codes, w_scales = codes[g]
+            cols = slice(s * SLICE, (s + 1) * SLICE)
+            nc.vector.quantize_mx(
+                out=w_codes[:, c, cols].bitcast(FP8X4),
+                scales=w_scales[:, c, cols],
+                in_=grouped.rearrange("p w j -> p (w j)"),
+            )
+
+        def multiply(g, s):
+            w_codes, w_scales = codes[g]
+            accs[(g, s)] = []
+            for pair in range(SLICE_TILES // 2):
+                acc = acc_psum.tile([P, 2, B], F32)
+                for half in range(2):
+                    t = s * SLICE_TILES + 2 * pair + half
+                    n_cols = slice(t * P, (t + 1) * P)
+                    for c in range(PASSES):
+                        nc.tensor.matmul_mx(
+                            out=acc[:, half, :],
+                            lhsT=w_codes[:, c, n_cols].bitcast(FP8X4),
+                            lhsT_scale=w_scales[:, c, n_cols],
+                            rhs=x_codes[:, c, :].bitcast(FP8X4),
+                            rhs_scale=x_scales[:, c, :],
+                            start=(c == 0),
+                            stop=(c == PASSES - 1),
+                        )
+                accs[(g, s)].append(acc)
+
+        def activate(g, s):
+            if g == 0:
+                gate = i_gate[:, s * SLICE_TILES : (s + 1) * SLICE_TILES, :]
+            else:
+                gate = work.tile([P, SLICE_TILES, B], F32, tag="gate")
+            for j in range(SLICE_TILES):
+                t = s * SLICE_TILES + j
+                nc.scalar.activation(
+                    out=gate[:, j, :],
+                    in_=accs[(g, s)][j // 2][:, j % 2, :],
+                    func=functions[g],
+                    bias=bias_cols[:, g * N_TILES + t : g * N_TILES + t + 1],
+                )
+            gates[(g, s)] = gate
+
+        def combine(g, s):
+            if g == 1:
+                state = work.tile([P, SLICE_TILES, B], F32, tag="state")
+                nc.vector.tensor_mul(out=state[:], in0=gates[(1, s)][:], in1=gates[(0, s)])
+                turned_banks[(g, s)] = turn_slice(nc, turn_psum, identity, state)
+            if g == 2:
+                turned_banks[(g, s)] = turn_slice(nc, turn_psum, identity, gates[(2, s)])
+
+        def finish(g, s):
+            cols = slice(s * SLICE, (s + 1) * SLICE)
+            if g == 1:
+                for a in range(M_TILES):
+                    nc.scalar.activation(
+                        out=tanh_state[:, a, cols], in_=turned_banks[(g, s)][a][:], func=ACT.Tanh
+                    )
+            if g == 2:
+                result = work.tile([P, M_TILES, SLICE], F32, tag="result")
+                for a in range(M_TILES):
+                    nc.vector.tensor_mul(
+                        out=result[:, a, :],
+                        in0=turned_banks[(g, s)][a][:],
+                        in1=tanh_state[:, a, cols],
+                    )
+                nc.sync.dma_start(out=out_view[:, :, cols], in_=result[:])
+
+        bias_rows = load_biases(nc, const, [bxi, bxc, bxo])
+        nc.sync.dma_start(
+            out=x_rows.rearrange("p (a k) -> p a k", a=M_TILES),
+            in_=x.rearrange("(a p) k -> p a k", p=P),
+        )
+        for k in range(RAW_BUFS):
+            load_pass(k)
+        bias_cols = turn_biases(nc, const, turn_psum, identity, bias_rows)
+        quantise_x(nc, grouped_pool, turn_psum, identity, x_rows, x_codes, x_scales)
+
+        units = unit_order()
+        regrouped = {}
+        complete = []
+        in_stage = [None, None, None, None]
+
+        entered = 0
+
+        step = 0
+        while step < len(units) + QUANTISE_LAG or entered < len(complete) or any(in_stage):
+            entering = complete[entered] if entered < len(complete) else None
+            entered += 1 if entering else 0
+            in_stage = [entering] + in_stage[:3]
+            if in_stage[0]:
+                multiply(*in_stage[0])
+            scalar_is_busier = any([item and item[0] < GATES - 1 for item in in_stage])
+            vector_cols = BUSY_VECTOR_COLS if scalar_is_busier else PLAIN_VECTOR_COLS
+            for spare in range(PERIOD):
+                if step < len(units):
+                    g, c, s = units[step]
+                    if c == 0 and s == 0:
+                        w_codes = quantised.tile([P, PASSES, D_OUT], U32, align_bytes=64)
+                        w_scales = quantised.tile([P, PASSES, D_OUT], U8, align_bytes=64)
+                        codes[g] = (w_codes, w_scales)
+                    regrouped[step] = regroup_slice(nc, grouped_pool, raws[(g, c)], s, vector_cols)
+                    k = g * PASSES + c + RAW_BUFS
+                    if s == SLICES - 1 and k < GATES * PASSES:
+                        load_pass(k)
+                if QUANTISE_LAG <= step < len(units) + QUANTISE_LAG:
+                    g, c, s = units[step - QUANTISE_LAG]
+                    quantise_unit(regrouped[step - QUANTISE_LAG], g, c, s)
+                    if c == PASSES - 1:
+                        complete.append((g, s))
+                step += 1
+            if in_stage[3]:
+                finish(*in_stage[3])
+            if in_stage[1]:
+                activate(*in_stage[1])
+            if in_stage[2]:
+                combine(*in_stage[2])

@@ -22,14 +22,14 @@ M_TILES = B // P
 N_TILES = D_OUT // P
 SLICE = 512
 SLICES = D_OUT // SLICE
-SLICE_TILES = SLICE // P
+PAIR = 2 * P
+PAIRS = D_OUT // PAIR
+SLICE_PAIRS = SLICE // PAIR
 
-PLAIN_VECTOR_COLS = 240
-BUSY_VECTOR_COLS = 336
+VECTOR_COLS = 280
 
-RAW_BUFS = 4
+RAW_BUFS = 5
 QUANTISE_LAG = 2
-PERIOD = 2
 
 FLOPS = 2 * B * D_IN * D_OUT * GATES
 
@@ -37,7 +37,7 @@ FLOPS = 2 * B * D_IN * D_OUT * GATES
 def unit_order():
     units = []
     for g in range(GATES):
-        by_pass = PASSES if g < GATES - 1 else PASSES // 2
+        by_pass = PASSES if g < GATES - 1 else 1
         units.extend([(g, c, s) for c in range(by_pass) for s in range(SLICES)])
         units.extend([(g, c, s) for s in range(SLICES) for c in range(by_pass, PASSES)])
     return units
@@ -85,32 +85,32 @@ def quantise_x(nc, grouped_pool, turn_psum, identity, x_rows, x_codes, x_scales)
         )
 
 
-def regroup_slice(nc, grouped_pool, raw, s, vector_cols):
+def regroup_slice(nc, grouped_pool, raw, s):
     grouped = grouped_pool.tile([P, SLICE, PACK], BF16, tag="grouped", align_bytes=64)
     first = s * SLICE
     nc.vector.tensor_copy(
-        out=grouped[:, :vector_cols, :].rearrange("p (r i) j -> p r j i", i=4),
-        in_=raw[:, :, first : first + vector_cols].rearrange("p j (r i) -> p r j i", i=4),
+        out=grouped[:, :VECTOR_COLS, :].rearrange("p (r i) j -> p r j i", i=4),
+        in_=raw[:, :, first : first + VECTOR_COLS].rearrange("p j (r i) -> p r j i", i=4),
     )
     nc.scalar.copy(
-        out=grouped[:, vector_cols:, :].rearrange("p (r i) j -> p r j i", i=4),
-        in_=raw[:, :, first + vector_cols : first + SLICE].rearrange(
+        out=grouped[:, VECTOR_COLS:, :].rearrange("p (r i) j -> p r j i", i=4),
+        in_=raw[:, :, first + VECTOR_COLS : first + SLICE].rearrange(
             "p j (r i) -> p r j i", i=4
         ),
     )
     return grouped
 
 
-def turn_slice(nc, turn_psum, identity, values):
-    banks = []
+def turn_pair(nc, turn_psum, identity, values):
+    bank = turn_psum.tile([P, M_TILES, PAIR], F32, tag="turned")
     for a in range(M_TILES):
-        bank = turn_psum.tile([P, SLICE], F32, tag="turned", name="bank")
-        for t in range(SLICE_TILES):
+        for half in range(2):
             nc.tensor.transpose(
-                bank[:, t * P : (t + 1) * P], values[:, t, a * P : (a + 1) * P], identity[:]
+                bank[:, a, half * P : (half + 1) * P],
+                values[:, half, a * P : (a + 1) * P],
+                identity[:],
             )
-        banks.append(bank)
-    return banks
+    return bank
 
 
 def tile_lstm_pa_kernel(tc, x, Wxi, bxi, Wxc, bxc, Wxo, bxo, out):
@@ -123,25 +123,24 @@ def tile_lstm_pa_kernel(tc, x, Wxi, bxi, Wxc, bxc, Wxo, bxo, out):
         ctx.enter_context(tc.manual_schedule())
         const = ctx.enter_context(tc.tile_pool(name="const", bufs=1))
         raw_pool = ctx.enter_context(tc.tile_pool(name="raw", bufs=RAW_BUFS))
-        grouped_pool = ctx.enter_context(tc.tile_pool(name="grouped", bufs=4))
+        grouped_pool = ctx.enter_context(tc.tile_pool(name="grouped", bufs=QUANTISE_LAG + 2))
         quantised = ctx.enter_context(tc.tile_pool(name="quantised", bufs=2))
-        work = ctx.enter_context(tc.tile_pool(name="work", bufs=2))
+        kept = ctx.enter_context(tc.tile_pool(name="kept", bufs=PAIRS))
+        work = ctx.enter_context(tc.tile_pool(name="work", bufs=3))
         acc_psum = ctx.enter_context(tc.psum_pool(name="acc", bufs=4))
         turn_psum = ctx.enter_context(tc.psum_pool(name="turn", bufs=4))
 
         identity = const.tile([P, P], F32)
         make_identity(nc, identity[:])
-        x_rows = const.tile([P, M_TILES * D_IN], BF16)
         x_codes = const.tile([P, PASSES, B], U32, align_bytes=64)
         x_scales = const.tile([P, PASSES, B], U8, align_bytes=64)
-        i_gate = const.tile([P, N_TILES, B], F32)
-        tanh_state = const.tile([P, M_TILES, D_OUT], F32)
 
         raws = {}
         codes = {}
         accs = {}
         gates = {}
         turned_banks = {}
+        tanh_states = {}
 
         def load_pass(k):
             g, c = divmod(k, PASSES)
@@ -163,112 +162,111 @@ def tile_lstm_pa_kernel(tc, x, Wxi, bxi, Wxc, bxc, Wxo, bxo, out):
                 in_=grouped.rearrange("p w j -> p (w j)"),
             )
 
-        def multiply(g, s):
+        def multiply(g, pair):
             w_codes, w_scales = codes[g]
-            accs[(g, s)] = []
-            for pair in range(SLICE_TILES // 2):
-                acc = acc_psum.tile([P, 2, B], F32)
-                for half in range(2):
-                    t = s * SLICE_TILES + 2 * pair + half
-                    n_cols = slice(t * P, (t + 1) * P)
-                    for c in range(PASSES):
-                        nc.tensor.matmul_mx(
-                            out=acc[:, half, :],
-                            lhsT=w_codes[:, c, n_cols].bitcast(FP8X4),
-                            lhsT_scale=w_scales[:, c, n_cols],
-                            rhs=x_codes[:, c, :].bitcast(FP8X4),
-                            rhs_scale=x_scales[:, c, :],
-                            start=(c == 0),
-                            stop=(c == PASSES - 1),
-                        )
-                accs[(g, s)].append(acc)
+            acc = acc_psum.tile([P, 2, B], F32)
+            for half in range(2):
+                t = 2 * pair + half
+                n_cols = slice(t * P, (t + 1) * P)
+                for c in range(PASSES):
+                    nc.tensor.matmul_mx(
+                        out=acc[:, half, :],
+                        lhsT=w_codes[:, c, n_cols].bitcast(FP8X4),
+                        lhsT_scale=w_scales[:, c, n_cols],
+                        rhs=x_codes[:, c, :].bitcast(FP8X4),
+                        rhs_scale=x_scales[:, c, :],
+                        start=(c == 0),
+                        stop=(c == PASSES - 1),
+                    )
+            accs[(g, pair)] = acc
 
-        def activate(g, s):
+        def activate(g, pair):
             if g == 0:
-                gate = i_gate[:, s * SLICE_TILES : (s + 1) * SLICE_TILES, :]
+                gate = kept.tile([P, 2, B], F32, tag="kept")
             else:
-                gate = work.tile([P, SLICE_TILES, B], F32, tag="gate")
-            for j in range(SLICE_TILES):
-                t = s * SLICE_TILES + j
+                gate = work.tile([P, 2, B], F32, tag="gate")
+            for half in range(2):
+                t = 2 * pair + half
                 nc.scalar.activation(
-                    out=gate[:, j, :],
-                    in_=accs[(g, s)][j // 2][:, j % 2, :],
+                    out=gate[:, half, :],
+                    in_=accs[(g, pair)][:, half, :],
                     func=functions[g],
                     bias=bias_cols[:, g * N_TILES + t : g * N_TILES + t + 1],
                 )
-            gates[(g, s)] = gate
+            gates[(g, pair)] = gate
 
-        def combine(g, s):
+        def combine(g, pair):
             if g == 1:
-                state = work.tile([P, SLICE_TILES, B], F32, tag="state")
-                nc.vector.tensor_mul(out=state[:], in0=gates[(1, s)][:], in1=gates[(0, s)])
-                turned_banks[(g, s)] = turn_slice(nc, turn_psum, identity, state)
+                state = work.tile([P, 2, B], F32, tag="state")
+                nc.vector.tensor_mul(
+                    out=state[:], in0=gates[(1, pair)][:], in1=gates[(0, pair)][:]
+                )
+                turned_banks[(g, pair)] = turn_pair(nc, turn_psum, identity, state)
             if g == 2:
-                turned_banks[(g, s)] = turn_slice(nc, turn_psum, identity, gates[(2, s)])
+                turned_banks[(g, pair)] = turn_pair(nc, turn_psum, identity, gates[(2, pair)])
 
-        def finish(g, s):
-            cols = slice(s * SLICE, (s + 1) * SLICE)
+        def finish(g, pair):
             if g == 1:
-                for a in range(M_TILES):
-                    nc.scalar.activation(
-                        out=tanh_state[:, a, cols], in_=turned_banks[(g, s)][a][:], func=ACT.Tanh
-                    )
+                tanh_state = kept.tile([P, M_TILES, PAIR], F32, tag="kept")
+                nc.scalar.activation(
+                    out=tanh_state[:], in_=turned_banks[(g, pair)][:], func=ACT.Tanh
+                )
+                tanh_states[pair] = tanh_state
             if g == 2:
-                result = work.tile([P, M_TILES, SLICE], F32, tag="result")
-                for a in range(M_TILES):
-                    nc.vector.tensor_mul(
-                        out=result[:, a, :],
-                        in0=turned_banks[(g, s)][a][:],
-                        in1=tanh_state[:, a, cols],
-                    )
-                nc.sync.dma_start(out=out_view[:, :, cols], in_=result[:])
+                result = work.tile([P, M_TILES, PAIR], F32, tag="result")
+                nc.vector.tensor_mul(
+                    out=result[:], in0=turned_banks[(g, pair)][:], in1=tanh_states[pair][:]
+                )
+                nc.sync.dma_start(
+                    out=out_view[:, :, pair * PAIR : (pair + 1) * PAIR], in_=result[:]
+                )
 
         bias_rows = load_biases(nc, const, [bxi, bxc, bxo])
+        x_rows = raw_pool.tile([P, M_TILES * D_IN], BF16, tag="raw")
         nc.sync.dma_start(
             out=x_rows.rearrange("p (a k) -> p a k", a=M_TILES),
             in_=x.rearrange("(a p) k -> p a k", p=P),
         )
-        for k in range(RAW_BUFS):
+        for k in range(RAW_BUFS - 1):
             load_pass(k)
         bias_cols = turn_biases(nc, const, turn_psum, identity, bias_rows)
         quantise_x(nc, grouped_pool, turn_psum, identity, x_rows, x_codes, x_scales)
+        load_pass(RAW_BUFS - 1)
 
         units = unit_order()
         regrouped = {}
         complete = []
-        in_stage = [None, None, None, None]
-
-        entered = 0
-
+        started = [None, None, None]
+        begun = 0
+        finished = 0
         step = 0
-        while step < len(units) + QUANTISE_LAG or entered < len(complete) or any(in_stage):
-            entering = complete[entered] if entered < len(complete) else None
-            entered += 1 if entering else 0
-            in_stage = [entering] + in_stage[:3]
-            if in_stage[0]:
-                multiply(*in_stage[0])
-            scalar_is_busier = any([item and item[0] < GATES - 1 for item in in_stage])
-            vector_cols = BUSY_VECTOR_COLS if scalar_is_busier else PLAIN_VECTOR_COLS
-            for spare in range(PERIOD):
-                if step < len(units):
-                    g, c, s = units[step]
-                    if c == 0 and s == 0:
-                        w_codes = quantised.tile([P, PASSES, D_OUT], U32, align_bytes=64)
-                        w_scales = quantised.tile([P, PASSES, D_OUT], U8, align_bytes=64)
-                        codes[g] = (w_codes, w_scales)
-                    regrouped[step] = regroup_slice(nc, grouped_pool, raws[(g, c)], s, vector_cols)
-                    k = g * PASSES + c + RAW_BUFS
-                    if s == SLICES - 1 and k < GATES * PASSES:
-                        load_pass(k)
-                if QUANTISE_LAG <= step < len(units) + QUANTISE_LAG:
-                    g, c, s = units[step - QUANTISE_LAG]
-                    quantise_unit(regrouped[step - QUANTISE_LAG], g, c, s)
-                    if c == PASSES - 1:
-                        complete.append((g, s))
-                step += 1
-            if in_stage[3]:
-                finish(*in_stage[3])
-            if in_stage[1]:
-                activate(*in_stage[1])
-            if in_stage[2]:
-                combine(*in_stage[2])
+        while finished < GATES * PAIRS:
+            if begun < len(complete):
+                started.append(complete[begun])
+                multiply(*complete[begun])
+                begun += 1
+            else:
+                started.append(None)
+            if step < len(units):
+                g, c, s = units[step]
+                if c == 0 and s == 0:
+                    w_codes = quantised.tile([P, PASSES, D_OUT], U32, align_bytes=64)
+                    w_scales = quantised.tile([P, PASSES, D_OUT], U8, align_bytes=64)
+                    codes[g] = (w_codes, w_scales)
+                regrouped[step] = regroup_slice(nc, grouped_pool, raws[(g, c)], s)
+                next_load = g * PASSES + c + RAW_BUFS
+                if s == SLICES - 1 and next_load < GATES * PASSES:
+                    load_pass(next_load)
+            if QUANTISE_LAG <= step < len(units) + QUANTISE_LAG:
+                g, c, s = units[step - QUANTISE_LAG]
+                quantise_unit(regrouped[step - QUANTISE_LAG], g, c, s)
+                if c == PASSES - 1:
+                    complete.extend([(g, s * SLICE_PAIRS + e) for e in range(SLICE_PAIRS)])
+            if started[-4]:
+                finish(*started[-4])
+                finished += 1
+            if started[-2]:
+                activate(*started[-2])
+            if started[-3]:
+                combine(*started[-3])
+            step += 1

@@ -26,7 +26,7 @@ PAIR = 2 * P
 PAIRS = D_OUT // PAIR
 SLICE_PAIRS = SLICE // PAIR
 
-VECTOR_COLS = 280
+VECTOR_COLS = 304
 
 RAW_BUFS = 5
 QUANTISE_LAG = 2

@@ -30,6 +30,8 @@ VECTOR_COLS = 304
 
 RAW_BUFS = 5
 QUANTISE_LAG = 2
+SPLIT_PASSES = 3
+X_FIRST_STEP = 3 * SLICES
 
 FLOPS = 2 * B * D_IN * D_OUT * GATES
 
@@ -64,39 +66,33 @@ def turn_biases(nc, const, turn_psum, identity, bias_rows):
     return bias_cols
 
 
-def quantise_x(nc, grouped_pool, turn_psum, identity, x_rows, x_codes, x_scales):
+def turn_x(nc, x_pool, turn_psum, identity, x_rows, c):
     x_words = x_rows[:].bitcast(F32).rearrange(
         "p (a c q u) -> p a c u q", a=M_TILES, c=PASSES, q=P, u=2
     )
-    for c in range(PASSES):
-        turned = turn_psum.tile([P, 2, B], F32, tag="turned")
-        for u in range(2):
-            for a in range(M_TILES):
-                nc.tensor.transpose(
-                    turned[:, u, a * P : (a + 1) * P], x_words[:, a, c, u, :], identity[:]
-                )
-        x_grouped = grouped_pool.tile([P, B * PACK], BF16, tag="grouped", align_bytes=64)
-        nc.scalar.copy(
-            out=x_grouped[:].bitcast(F32).rearrange("p (m u) -> p m u", u=2),
-            in_=turned.rearrange("p u m -> p m u"),
-        )
-        nc.vector.quantize_mx(
-            out=x_codes[:, c, :].bitcast(FP8X4), scales=x_scales[:, c, :], in_=x_grouped[:]
-        )
+    turned = turn_psum.tile([P, 2, B], F32, tag="turned")
+    for u in range(2):
+        for a in range(M_TILES):
+            nc.tensor.transpose(
+                turned[:, u, a * P : (a + 1) * P], x_words[:, a, c, u, :], identity[:]
+            )
+    x_grouped = x_pool.tile([P, B * PACK], BF16, tag="x_grouped", align_bytes=64)
+    nc.scalar.copy(
+        out=x_grouped[:].bitcast(F32).rearrange("p (m u) -> p m u", u=2),
+        in_=turned.rearrange("p u m -> p m u"),
+    )
+    return x_grouped
 
 
-def regroup_slice(nc, grouped_pool, raw, s):
+def regroup_slice(nc, grouped_pool, raw_slice):
     grouped = grouped_pool.tile([P, SLICE, PACK], BF16, tag="grouped", align_bytes=64)
-    first = s * SLICE
     nc.vector.tensor_copy(
         out=grouped[:, :VECTOR_COLS, :].rearrange("p (r i) j -> p r j i", i=4),
-        in_=raw[:, :, first : first + VECTOR_COLS].rearrange("p j (r i) -> p r j i", i=4),
+        in_=raw_slice[:, :, :VECTOR_COLS].rearrange("p j (r i) -> p r j i", i=4),
     )
     nc.scalar.copy(
         out=grouped[:, VECTOR_COLS:, :].rearrange("p (r i) j -> p r j i", i=4),
-        in_=raw[:, :, first + VECTOR_COLS : first + SLICE].rearrange(
-            "p j (r i) -> p r j i", i=4
-        ),
+        in_=raw_slice[:, :, VECTOR_COLS:].rearrange("p j (r i) -> p r j i", i=4),
     )
     return grouped
 
@@ -124,11 +120,17 @@ def tile_lstm_pa_kernel(tc, x, Wxi, bxi, Wxc, bxc, Wxo, bxo, out):
         const = ctx.enter_context(tc.tile_pool(name="const", bufs=1))
         raw_pool = ctx.enter_context(tc.tile_pool(name="raw", bufs=RAW_BUFS))
         grouped_pool = ctx.enter_context(tc.tile_pool(name="grouped", bufs=QUANTISE_LAG + 2))
+        x_pool = ctx.enter_context(tc.tile_pool(name="x_grouped", bufs=2))
         quantised = ctx.enter_context(tc.tile_pool(name="quantised", bufs=2))
         kept = ctx.enter_context(tc.tile_pool(name="kept", bufs=PAIRS))
         work = ctx.enter_context(tc.tile_pool(name="work", bufs=3))
         acc_psum = ctx.enter_context(tc.psum_pool(name="acc", bufs=4))
         turn_psum = ctx.enter_context(tc.psum_pool(name="turn", bufs=4))
+
+        table_in = const.tile([P, 1], F32)
+        table_out = const.tile([P, 1], F32)
+        nc.vector.memset(table_in[:], 0.0)
+        nc.scalar.activation(out=table_out[:], in_=table_in[:], func=ACT.Sigmoid)
 
         identity = const.tile([P, P], F32)
         make_identity(nc, identity[:])
@@ -144,14 +146,22 @@ def tile_lstm_pa_kernel(tc, x, Wxi, bxi, Wxc, bxc, Wxo, bxo, out):
 
         def load_pass(k):
             g, c = divmod(k, PASSES)
-            raw = raw_pool.tile([P, PACK, D_OUT], BF16, tag="raw")
-            nc.sync.dma_start(
-                out=raw[:],
-                in_=weights[g][c * K_PASS : (c + 1) * K_PASS, :].rearrange(
-                    "(p j) w -> p j w", j=PACK
-                ),
+            rows = weights[g][c * K_PASS : (c + 1) * K_PASS, :].rearrange(
+                "(p j) w -> p j w", j=PACK
             )
-            raws[(g, c)] = raw
+            if k < SPLIT_PASSES:
+                raw_split = raw_pool.tile([P, SLICES, PACK, SLICE], BF16, tag="raw")
+                for s in range(SLICES):
+                    nc.sync.dma_start(
+                        out=raw_split[:, s, :, :], in_=rows[:, :, s * SLICE : (s + 1) * SLICE]
+                    )
+                raws[(g, c)] = [raw_split[:, s, :, :] for s in range(SLICES)]
+            else:
+                raw = raw_pool.tile([P, PACK, D_OUT], BF16, tag="raw")
+                nc.sync.dma_start(out=raw[:], in_=rows)
+                raws[(g, c)] = [
+                    raw[:, :, s * SLICE : (s + 1) * SLICE] for s in range(SLICES)
+                ]
 
         def quantise_unit(grouped, g, c, s):
             w_codes, w_scales = codes[g]
@@ -221,27 +231,28 @@ def tile_lstm_pa_kernel(tc, x, Wxi, bxi, Wxc, bxc, Wxo, bxo, out):
                     out=out_view[:, :, pair * PAIR : (pair + 1) * PAIR], in_=result[:]
                 )
 
+        for k in range(PASSES):
+            load_pass(k)
         bias_rows = load_biases(nc, const, [bxi, bxc, bxo])
-        x_rows = raw_pool.tile([P, M_TILES * D_IN], BF16, tag="raw")
+        x_rows = const.tile([P, M_TILES * D_IN], BF16)
         nc.sync.dma_start(
             out=x_rows.rearrange("p (a k) -> p a k", a=M_TILES),
             in_=x.rearrange("(a p) k -> p a k", p=P),
         )
-        for k in range(RAW_BUFS - 1):
+        for k in range(PASSES, RAW_BUFS):
             load_pass(k)
-        bias_cols = turn_biases(nc, const, turn_psum, identity, bias_rows)
-        quantise_x(nc, grouped_pool, turn_psum, identity, x_rows, x_codes, x_scales)
-        load_pass(RAW_BUFS - 1)
 
         units = unit_order()
         regrouped = {}
+        x_grouped = {}
+        bias_cols = None
         complete = []
         started = [None, None, None]
         begun = 0
         finished = 0
         step = 0
         while finished < GATES * PAIRS:
-            if begun < len(complete):
+            if begun < len(complete) and step > X_FIRST_STEP + PASSES:
                 started.append(complete[begun])
                 multiply(*complete[begun])
                 begun += 1
@@ -253,7 +264,7 @@ def tile_lstm_pa_kernel(tc, x, Wxi, bxi, Wxc, bxc, Wxo, bxo, out):
                     w_codes = quantised.tile([P, PASSES, D_OUT], U32, align_bytes=64)
                     w_scales = quantised.tile([P, PASSES, D_OUT], U8, align_bytes=64)
                     codes[g] = (w_codes, w_scales)
-                regrouped[step] = regroup_slice(nc, grouped_pool, raws[(g, c)], s)
+                regrouped[step] = regroup_slice(nc, grouped_pool, raws[(g, c)][s])
                 next_load = g * PASSES + c + RAW_BUFS
                 if s == SLICES - 1 and next_load < GATES * PASSES:
                     load_pass(next_load)
@@ -262,6 +273,18 @@ def tile_lstm_pa_kernel(tc, x, Wxi, bxi, Wxc, bxc, Wxo, bxo, out):
                 quantise_unit(regrouped[step - QUANTISE_LAG], g, c, s)
                 if c == PASSES - 1:
                     complete.extend([(g, s * SLICE_PAIRS + e) for e in range(SLICE_PAIRS)])
+            if step == X_FIRST_STEP:
+                bias_cols = turn_biases(nc, const, turn_psum, identity, bias_rows)
+            if 0 <= step - X_FIRST_STEP < PASSES:
+                c = step - X_FIRST_STEP
+                x_grouped[c] = turn_x(nc, x_pool, turn_psum, identity, x_rows, c)
+            if 0 <= step - X_FIRST_STEP - 1 < PASSES:
+                c = step - X_FIRST_STEP - 1
+                nc.vector.quantize_mx(
+                    out=x_codes[:, c, :].bitcast(FP8X4),
+                    scales=x_scales[:, c, :],
+                    in_=x_grouped[c][:],
+                )
             if started[-4]:
                 finish(*started[-4])
                 finished += 1

@@ -26,7 +26,8 @@ PAIR = 2 * P
 PAIRS = D_OUT // PAIR
 SLICE_PAIRS = SLICE // PAIR
 
-VECTOR_COLS = 304
+BASE_COLS = 248
+PASS_COLS = 88
 
 RAW_BUFS = 5
 QUANTISE_LAG = 2
@@ -84,15 +85,15 @@ def turn_x(nc, x_pool, turn_psum, identity, x_rows, c):
     return x_grouped
 
 
-def regroup_slice(nc, grouped_pool, raw_slice):
+def regroup_slice(nc, grouped_pool, raw_slice, vector_cols):
     grouped = grouped_pool.tile([P, SLICE, PACK], BF16, tag="grouped", align_bytes=64)
     nc.vector.tensor_copy(
-        out=grouped[:, :VECTOR_COLS, :].rearrange("p (r i) j -> p r j i", i=4),
-        in_=raw_slice[:, :, :VECTOR_COLS].rearrange("p j (r i) -> p r j i", i=4),
+        out=grouped[:, :vector_cols, :].rearrange("p (r i) j -> p r j i", i=4),
+        in_=raw_slice[:, :, :vector_cols].rearrange("p j (r i) -> p r j i", i=4),
     )
     nc.scalar.copy(
-        out=grouped[:, VECTOR_COLS:, :].rearrange("p (r i) j -> p r j i", i=4),
-        in_=raw_slice[:, :, VECTOR_COLS:].rearrange("p j (r i) -> p r j i", i=4),
+        out=grouped[:, vector_cols:, :].rearrange("p (r i) j -> p r j i", i=4),
+        in_=raw_slice[:, :, vector_cols:].rearrange("p j (r i) -> p r j i", i=4),
     )
     return grouped
 
@@ -264,7 +265,25 @@ def tile_lstm_pa_kernel(tc, x, Wxi, bxi, Wxc, bxc, Wxo, bxo, out):
                     w_codes = quantised.tile([P, PASSES, D_OUT], U32, align_bytes=64)
                     w_scales = quantised.tile([P, PASSES, D_OUT], U8, align_bytes=64)
                     codes[g] = (w_codes, w_scales)
-                regrouped[step] = regroup_slice(nc, grouped_pool, raws[(g, c)][s])
+                scalar_passes = sum(
+                    [
+                        bool(started[-2]),
+                        bool(started[-4]) and started[-4][0] == 1,
+                        0 <= step - X_FIRST_STEP < PASSES,
+                    ]
+                )
+                vector_passes = sum(
+                    [
+                        bool(started[-3]) and started[-3][0] == 1,
+                        bool(started[-4]) and started[-4][0] == 2,
+                    ]
+                )
+                regrouped[step] = regroup_slice(
+                    nc,
+                    grouped_pool,
+                    raws[(g, c)][s],
+                    BASE_COLS + PASS_COLS * (scalar_passes - vector_passes),
+                )
                 next_load = g * PASSES + c + RAW_BUFS
                 if s == SLICES - 1 and next_load < GATES * PASSES:
                     load_pass(next_load)

@@ -20,19 +20,22 @@ GATES = 3
 PASSES = D_IN // K_PASS
 M_TILES = B // P
 N_TILES = D_OUT // P
-SLICE = 512
-SLICES = D_OUT // SLICE
 PAIR = 2 * P
 PAIRS = D_OUT // PAIR
-SLICE_PAIRS = SLICE // PAIR
+LAST_PAIR = (GATES - 1, PAIRS - 1)
 
-BASE_COLS = 248
+SLICE = 512
+
+BASE_COLS = 232
 PASS_COLS = 88
+PAIR_VECTOR_COLS = 168
 
 RAW_BUFS = 5
 QUANTISE_LAG = 2
-SPLIT_PASSES = 3
-X_FIRST_STEP = 3 * SLICES
+FIRST_PART = SLICE
+FIRST_PASSES = 6
+PART = 2 * SLICE
+X_BEHIND = 5
 
 FLOPS = 2 * B * D_IN * D_OUT * GATES
 
@@ -41,8 +44,12 @@ def unit_order():
     units = []
     for g in range(GATES):
         by_pass = PASSES if g < GATES - 1 else 1
-        units.extend([(g, c, s) for c in range(by_pass) for s in range(SLICES)])
-        units.extend([(g, c, s) for s in range(SLICES) for c in range(by_pass, PASSES)])
+        for c in range(by_pass):
+            units.extend([(g, c, first, SLICE) for first in range(0, D_OUT, SLICE)])
+        for first in range(0, D_OUT - SLICE, SLICE):
+            units.extend([(g, c, first, SLICE) for c in range(by_pass, PASSES)])
+        for first in range(D_OUT - SLICE, D_OUT, PAIR):
+            units.extend([(g, c, first, PAIR) for c in range(by_pass, PASSES)])
     return units
 
 
@@ -85,23 +92,23 @@ def turn_x(nc, x_pool, turn_psum, identity, x_rows, c):
     return x_grouped
 
 
-def regroup_slice(nc, grouped_pool, raw_slice, vector_cols):
-    grouped = grouped_pool.tile([P, SLICE, PACK], BF16, tag="grouped", align_bytes=64)
+def regroup(nc, grouped_pool, raw_cols, width, vector_cols):
+    grouped = grouped_pool.tile([P, width, PACK], BF16, tag="grouped", align_bytes=64)
     nc.vector.tensor_copy(
         out=grouped[:, :vector_cols, :].rearrange("p (r i) j -> p r j i", i=4),
-        in_=raw_slice[:, :, :vector_cols].rearrange("p j (r i) -> p r j i", i=4),
+        in_=raw_cols[:, :, :vector_cols].rearrange("p j (r i) -> p r j i", i=4),
     )
     nc.scalar.copy(
         out=grouped[:, vector_cols:, :].rearrange("p (r i) j -> p r j i", i=4),
-        in_=raw_slice[:, :, vector_cols:].rearrange("p j (r i) -> p r j i", i=4),
+        in_=raw_cols[:, :, vector_cols:].rearrange("p j (r i) -> p r j i", i=4),
     )
     return grouped
 
 
 def turn_pair(nc, turn_psum, identity, values):
     bank = turn_psum.tile([P, M_TILES, PAIR], F32, tag="turned")
-    for a in range(M_TILES):
-        for half in range(2):
+    for half in range(2):
+        for a in range(M_TILES):
             nc.tensor.transpose(
                 bank[:, a, half * P : (half + 1) * P],
                 values[:, half, a * P : (a + 1) * P],
@@ -145,51 +152,79 @@ def tile_lstm_pa_kernel(tc, x, Wxi, bxi, Wxc, bxc, Wxo, bxo, out):
         turned_banks = {}
         tanh_states = {}
 
-        def load_pass(k):
-            g, c = divmod(k, PASSES)
-            rows = weights[g][c * K_PASS : (c + 1) * K_PASS, :].rearrange(
-                "(p j) w -> p j w", j=PACK
-            )
-            if k < SPLIT_PASSES:
-                raw_split = raw_pool.tile([P, SLICES, PACK, SLICE], BF16, tag="raw")
-                for s in range(SLICES):
-                    nc.sync.dma_start(
-                        out=raw_split[:, s, :, :], in_=rows[:, :, s * SLICE : (s + 1) * SLICE]
-                    )
-                raws[(g, c)] = [raw_split[:, s, :, :] for s in range(SLICES)]
-            else:
-                raw = raw_pool.tile([P, PACK, D_OUT], BF16, tag="raw")
-                nc.sync.dma_start(out=raw[:], in_=rows)
-                raws[(g, c)] = [
-                    raw[:, :, s * SLICE : (s + 1) * SLICE] for s in range(SLICES)
-                ]
+        def part_width(k):
+            return FIRST_PART if k < FIRST_PASSES else PART
 
-        def quantise_unit(grouped, g, c, s):
+        def load_part(k, e):
+            g, c = divmod(k, PASSES)
+            width = part_width(k)
+            nc.sync.dma_start(
+                out=raws[k][:, e, :, :],
+                in_=weights[g][
+                    c * K_PASS : (c + 1) * K_PASS, e * width : (e + 1) * width
+                ].rearrange("(p j) w -> p j w", j=PACK),
+            )
+
+        def load_pass(k):
+            parts = D_OUT // part_width(k)
+            raw = raw_pool.tile([P, parts, PACK, part_width(k)], BF16, tag="raw")
+            raws[k] = raw
+            by_columns = range((GATES - 1) * PASSES + 1, GATES * PASSES)
+            if k not in by_columns:
+                for e in range(parts):
+                    load_part(k, e)
+                return
+            load_part(k, 0)
+            if k == by_columns[-1]:
+                for e in range(1, parts):
+                    for k_late in by_columns:
+                        load_part(k_late, e)
+
+        def unit_cols(g, c, first, width):
+            k = g * PASSES + c
+            inside = first % part_width(k)
+            return raws[k][:, first // part_width(k), :, inside : inside + width]
+
+        def quantise_unit(grouped, g, c, first, width):
             w_codes, w_scales = codes[g]
-            cols = slice(s * SLICE, (s + 1) * SLICE)
             nc.vector.quantize_mx(
-                out=w_codes[:, c, cols].bitcast(FP8X4),
-                scales=w_scales[:, c, cols],
+                out=w_codes[:, c, first : first + width].bitcast(FP8X4),
+                scales=w_scales[:, c, first : first + width],
                 in_=grouped.rearrange("p w j -> p (w j)"),
             )
 
-        def multiply(g, pair):
+        def multiply_pass(g, pair, half, c):
             w_codes, w_scales = codes[g]
-            acc = acc_psum.tile([P, 2, B], F32)
+            t = 2 * pair + half
+            nc.tensor.matmul_mx(
+                out=accs[(g, pair)][half],
+                lhsT=w_codes[:, c, t * P : (t + 1) * P].bitcast(FP8X4),
+                lhsT_scale=w_scales[:, c, t * P : (t + 1) * P],
+                rhs=x_codes[:, c, :].bitcast(FP8X4),
+                rhs_scale=x_scales[:, c, :],
+                start=(c == 0),
+                stop=(c == PASSES - 1),
+            )
+
+        def multiply(g, pair):
+            if (g, pair) == LAST_PAIR:
+                multiply_last_pair(PASSES - 1)
+                return
+            acc = acc_psum.tile([P, 2, B], F32, tag="acc")
+            accs[(g, pair)] = [acc[:, half, :] for half in range(2)]
             for half in range(2):
-                t = 2 * pair + half
-                n_cols = slice(t * P, (t + 1) * P)
                 for c in range(PASSES):
-                    nc.tensor.matmul_mx(
-                        out=acc[:, half, :],
-                        lhsT=w_codes[:, c, n_cols].bitcast(FP8X4),
-                        lhsT_scale=w_scales[:, c, n_cols],
-                        rhs=x_codes[:, c, :].bitcast(FP8X4),
-                        rhs_scale=x_scales[:, c, :],
-                        start=(c == 0),
-                        stop=(c == PASSES - 1),
-                    )
-            accs[(g, pair)] = acc
+                    multiply_pass(g, pair, half, c)
+
+        def multiply_last_pair(c):
+            if c == 1:
+                acc_0 = acc_psum.tile([P, B], F32, tag="acc")
+                acc_1 = acc_psum.tile([P, B], F32, tag="acc")
+                accs[LAST_PAIR] = [acc_0[:], acc_1[:]]
+                for half in range(2):
+                    multiply_pass(*LAST_PAIR, half, 0)
+            for half in range(2):
+                multiply_pass(*LAST_PAIR, half, c)
 
         def activate(g, pair):
             if g == 0:
@@ -200,7 +235,7 @@ def tile_lstm_pa_kernel(tc, x, Wxi, bxi, Wxc, bxc, Wxo, bxo, out):
                 t = 2 * pair + half
                 nc.scalar.activation(
                     out=gate[:, half, :],
-                    in_=accs[(g, pair)][:, half, :],
+                    in_=accs[(g, pair)][half],
                     func=functions[g],
                     bias=bias_cols[:, g * N_TILES + t : g * N_TILES + t + 1],
                 )
@@ -232,7 +267,7 @@ def tile_lstm_pa_kernel(tc, x, Wxi, bxi, Wxc, bxc, Wxo, bxo, out):
                     out=out_view[:, :, pair * PAIR : (pair + 1) * PAIR], in_=result[:]
                 )
 
-        for k in range(PASSES):
+        for k in range(X_BEHIND):
             load_pass(k)
         bias_rows = load_biases(nc, const, [bxi, bxc, bxo])
         x_rows = const.tile([P, M_TILES * D_IN], BF16)
@@ -240,75 +275,84 @@ def tile_lstm_pa_kernel(tc, x, Wxi, bxi, Wxc, bxc, Wxo, bxo, out):
             out=x_rows.rearrange("p (a k) -> p a k", a=M_TILES),
             in_=x.rearrange("(a p) k -> p a k", p=P),
         )
-        for k in range(PASSES, RAW_BUFS):
+        for k in range(X_BEHIND, RAW_BUFS):
             load_pass(k)
 
         units = unit_order()
+        x_first_step = units.index((X_BEHIND // PASSES, X_BEHIND % PASSES, 0, SLICE))
         regrouped = {}
         x_grouped = {}
         bias_cols = None
         complete = []
-        started = [None, None, None]
+        started = [[], [], []]
+        last_pair_pass = 0
         begun = 0
         finished = 0
         step = 0
         while finished < GATES * PAIRS:
-            if begun < len(complete) and step > X_FIRST_STEP + PASSES:
-                started.append(complete[begun])
-                multiply(*complete[begun])
-                begun += 1
-            else:
-                started.append(None)
+            batch = []
+            if step > x_first_step + PASSES:
+                batch = complete[begun : begun + 1]
+            begun += len(batch)
+            started.append(batch)
+            for pair in batch:
+                multiply(*pair)
+            if last_pair_pass:
+                multiply_last_pair(last_pair_pass)
+                last_pair_pass = 0
             if step < len(units):
-                g, c, s = units[step]
-                if c == 0 and s == 0:
+                g, c, first, width = units[step]
+                if c == 0 and first == 0:
                     w_codes = quantised.tile([P, PASSES, D_OUT], U32, align_bytes=64)
                     w_scales = quantised.tile([P, PASSES, D_OUT], U8, align_bytes=64)
                     codes[g] = (w_codes, w_scales)
-                scalar_passes = sum(
-                    [
-                        bool(started[-2]),
-                        bool(started[-4]) and started[-4][0] == 1,
-                        0 <= step - X_FIRST_STEP < PASSES,
-                    ]
+                scalar_passes = (
+                    len(started[-2])
+                    + len([pair for pair in started[-4] if pair[0] == 1])
+                    + (0 <= step - x_first_step < PASSES)
                 )
-                vector_passes = sum(
-                    [
-                        bool(started[-3]) and started[-3][0] == 1,
-                        bool(started[-4]) and started[-4][0] == 2,
-                    ]
+                vector_passes = len([pair for pair in started[-3] if pair[0] == 1]) + len(
+                    [pair for pair in started[-4] if pair[0] == 2]
                 )
-                regrouped[step] = regroup_slice(
+                vector_cols = BASE_COLS + PASS_COLS * (scalar_passes - vector_passes)
+                if width == PAIR:
+                    vector_cols = PAIR_VECTOR_COLS
+                regrouped[step] = regroup(
                     nc,
                     grouped_pool,
-                    raws[(g, c)][s],
-                    BASE_COLS + PASS_COLS * (scalar_passes - vector_passes),
+                    unit_cols(g, c, first, width),
+                    width,
+                    vector_cols,
                 )
                 next_load = g * PASSES + c + RAW_BUFS
-                if s == SLICES - 1 and next_load < GATES * PASSES:
+                if first + width == D_OUT and next_load < GATES * PASSES:
                     load_pass(next_load)
             if QUANTISE_LAG <= step < len(units) + QUANTISE_LAG:
-                g, c, s = units[step - QUANTISE_LAG]
-                quantise_unit(regrouped[step - QUANTISE_LAG], g, c, s)
+                g, c, first, width = units[step - QUANTISE_LAG]
+                quantise_unit(regrouped[step - QUANTISE_LAG], g, c, first, width)
                 if c == PASSES - 1:
-                    complete.extend([(g, s * SLICE_PAIRS + e) for e in range(SLICE_PAIRS)])
-            if step == X_FIRST_STEP:
+                    complete.extend(
+                        [(g, pair) for pair in range(first // PAIR, (first + width) // PAIR)]
+                    )
+                elif (g, first // PAIR) == LAST_PAIR and c > 0:
+                    last_pair_pass = c
+            if step == x_first_step:
                 bias_cols = turn_biases(nc, const, turn_psum, identity, bias_rows)
-            if 0 <= step - X_FIRST_STEP < PASSES:
-                c = step - X_FIRST_STEP
+            if 0 <= step - x_first_step < PASSES:
+                c = step - x_first_step
                 x_grouped[c] = turn_x(nc, x_pool, turn_psum, identity, x_rows, c)
-            if 0 <= step - X_FIRST_STEP - 1 < PASSES:
-                c = step - X_FIRST_STEP - 1
+            if 0 <= step - x_first_step - 1 < PASSES:
+                c = step - x_first_step - 1
                 nc.vector.quantize_mx(
                     out=x_codes[:, c, :].bitcast(FP8X4),
                     scales=x_scales[:, c, :],
                     in_=x_grouped[c][:],
                 )
-            if started[-4]:
-                finish(*started[-4])
+            for pair in started[-4]:
+                finish(*pair)
                 finished += 1
-            if started[-2]:
-                activate(*started[-2])
-            if started[-3]:
-                combine(*started[-3])
+            for pair in started[-2]:
+                activate(*pair)
+            for pair in started[-3]:
+                combine(*pair)
             step += 1

@@ -26,7 +26,7 @@ LAST_PAIR = (GATES - 1, PAIRS - 1)
 
 SLICE = 512
 
-BASE_COLS = 232
+BASE_COLS = 248
 PASS_COLS = 88
 PAIR_VECTOR_COLS = 168
 

@@ -33,7 +33,7 @@ PAIR_VECTOR_COLS = 168
 RAW_BUFS = 5
 QUANTISE_LAG = 2
 FIRST_PART = SLICE
-FIRST_PASSES = 6
+FIRST_PASSES = 8
 PART = 2 * SLICE
 X_BEHIND = 5
 
@@ -53,15 +53,12 @@ def unit_order():
     return units
 
 
-def load_biases(nc, const, biases):
-    bias_rows = const.tile([P, P], BF16)
-    nc.vector.memset(bias_rows[:].bitcast(I32), 0)
+def load_biases(nc, bias_rows, biases):
     for g in range(GATES):
         nc.sync.dma_start(
             out=bias_rows[g * N_TILES : (g + 1) * N_TILES, :],
             in_=biases[g].rearrange("(t n) -> t n", n=P),
         )
-    return bias_rows
 
 
 def turn_biases(nc, const, turn_psum, identity, bias_rows):
@@ -76,7 +73,7 @@ def turn_biases(nc, const, turn_psum, identity, bias_rows):
 
 def turn_x(nc, x_pool, turn_psum, identity, x_rows, c):
     x_words = x_rows[:].bitcast(F32).rearrange(
-        "p (a c q u) -> p a c u q", a=M_TILES, c=PASSES, q=P, u=2
+        "p (c a q u) -> p a c u q", a=M_TILES, c=PASSES, q=P, u=2
     )
     turned = turn_psum.tile([P, 2, B], F32, tag="turned")
     for u in range(2):
@@ -152,6 +149,12 @@ def tile_lstm_pa_kernel(tc, x, Wxi, bxi, Wxc, bxc, Wxo, bxo, out):
         turned_banks = {}
         tanh_states = {}
 
+        def load_x(c):
+            nc.sync.dma_start(
+                out=x_rows.rearrange("p (c a k) -> p c a k", c=PASSES, a=M_TILES)[:, c, :, :],
+                in_=x.rearrange("(a p) k -> p a k", p=P)[:, :, c * K_PASS : (c + 1) * K_PASS],
+            )
+
         def part_width(k):
             return FIRST_PART if k < FIRST_PASSES else PART
 
@@ -173,6 +176,10 @@ def tile_lstm_pa_kernel(tc, x, Wxi, bxi, Wxc, bxc, Wxo, bxo, out):
             if k not in by_columns:
                 for e in range(parts):
                     load_part(k, e)
+                    if k == X_BEHIND and e + 1 < PASSES:
+                        load_x(e + 1)
+                if k == X_BEHIND:
+                    load_biases(nc, bias_rows, [bxi, bxc, bxo])
                 return
             load_part(k, 0)
             if k == by_columns[-1]:
@@ -267,16 +274,12 @@ def tile_lstm_pa_kernel(tc, x, Wxi, bxi, Wxc, bxc, Wxo, bxo, out):
                     out=out_view[:, :, pair * PAIR : (pair + 1) * PAIR], in_=result[:]
                 )
 
-        for k in range(X_BEHIND):
-            load_pass(k)
-        bias_rows = load_biases(nc, const, [bxi, bxc, bxo])
+        bias_rows = const.tile([P, P], BF16)
+        nc.vector.memset(bias_rows[:].bitcast(I32), 0)
         x_rows = const.tile([P, M_TILES * D_IN], BF16)
-        nc.sync.dma_start(
-            out=x_rows.rearrange("p (a k) -> p a k", a=M_TILES),
-            in_=x.rearrange("(a p) k -> p a k", p=P),
-        )
-        for k in range(X_BEHIND, RAW_BUFS):
+        for k in range(RAW_BUFS):
             load_pass(k)
+        load_x(0)
 
         units = unit_order()
         x_first_step = units.index((X_BEHIND // PASSES, X_BEHIND % PASSES, 0, SLICE))
@@ -336,7 +339,7 @@ def tile_lstm_pa_kernel(tc, x, Wxi, bxi, Wxc, bxc, Wxo, bxo, out):
                     )
                 elif (g, first // PAIR) == LAST_PAIR and c > 0:
                     last_pair_pass = c
-            if step == x_first_step:
+            if step == x_first_step + PASSES:
                 bias_cols = turn_biases(nc, const, turn_psum, identity, bias_rows)
             if 0 <= step - x_first_step < PASSES:
                 c = step - x_first_step

@@ -30,6 +30,10 @@ BASE_COLS = 248
 PASS_COLS = 88
 PAIR_VECTOR_COLS = 168
 
+WARM_STEPS = 2
+WARM_COLS = 512
+WARM_MATMULS = 2
+
 RAW_BUFS = 5
 QUANTISE_LAG = 2
 FIRST_PART = SLICE
@@ -55,7 +59,7 @@ def unit_order():
 
 def load_biases(nc, bias_rows, biases):
     for g in range(GATES):
-        nc.sync.dma_start(
+        nc.scalar.dma_start(
             out=bias_rows[g * N_TILES : (g + 1) * N_TILES, :],
             in_=biases[g].rearrange("(t n) -> t n", n=P),
         )
@@ -178,8 +182,6 @@ def tile_lstm_pa_kernel(tc, x, Wxi, bxi, Wxc, bxc, Wxo, bxo, out):
                     load_part(k, e)
                     if k == X_BEHIND and e + 1 < PASSES:
                         load_x(e + 1)
-                if k == X_BEHIND:
-                    load_biases(nc, bias_rows, [bxi, bxc, bxo])
                 return
             load_part(k, 0)
             if k == by_columns[-1]:
@@ -276,6 +278,7 @@ def tile_lstm_pa_kernel(tc, x, Wxi, bxi, Wxc, bxc, Wxo, bxo, out):
 
         bias_rows = const.tile([P, P], BF16)
         nc.vector.memset(bias_rows[:].bitcast(I32), 0)
+        load_biases(nc, bias_rows, [bxi, bxc, bxo])
         x_rows = const.tile([P, M_TILES * D_IN], BF16)
         for k in range(RAW_BUFS):
             load_pass(k)
@@ -303,6 +306,16 @@ def tile_lstm_pa_kernel(tc, x, Wxi, bxi, Wxc, bxc, Wxo, bxo, out):
             if last_pair_pass:
                 multiply_last_pair(last_pair_pass)
                 last_pair_pass = 0
+            if 0 <= x_first_step + PASSES - step < WARM_STEPS:
+                warm_bank = turn_psum.tile([P, WARM_COLS], F32, tag="turned")
+                for repeat in range(WARM_MATMULS):
+                    nc.tensor.matmul(
+                        out=warm_bank[:],
+                        lhsT=x_rows[:, :P],
+                        rhs=x_rows[:, :WARM_COLS],
+                        start=True,
+                        stop=True,
+                    )
             if step < len(units):
                 g, c, first, width = units[step]
                 if c == 0 and first == 0:

@@ -23,6 +23,7 @@ N_TILES = D_OUT // P
 PAIR = 2 * P
 PAIRS = D_OUT // PAIR
 LAST_PAIR = (GATES - 1, PAIRS - 1)
+EARLY = [5, 6, 7]
 
 SLICE = 512
 
@@ -216,8 +217,8 @@ def tile_lstm_pa_kernel(tc, x, Wxi, bxi, Wxc, bxc, Wxo, bxo, out):
             )
 
         def multiply(g, pair):
-            if (g, pair) == LAST_PAIR:
-                multiply_last_pair(PASSES - 1)
+            if g == GATES - 1 and pair in EARLY:
+                multiply_early(pair, PASSES - 1)
                 return
             acc = acc_psum.tile([P, 2, B], F32, tag="acc")
             accs[(g, pair)] = [acc[:, half, :] for half in range(2)]
@@ -225,15 +226,16 @@ def tile_lstm_pa_kernel(tc, x, Wxi, bxi, Wxc, bxc, Wxo, bxo, out):
                 for c in range(PASSES):
                     multiply_pass(g, pair, half, c)
 
-        def multiply_last_pair(c):
+        def multiply_early(pair, c):
+            g = GATES - 1
             if c == 1:
                 acc_0 = acc_psum.tile([P, B], F32, tag="acc")
                 acc_1 = acc_psum.tile([P, B], F32, tag="acc")
-                accs[LAST_PAIR] = [acc_0[:], acc_1[:]]
+                accs[(g, pair)] = [acc_0[:], acc_1[:]]
                 for half in range(2):
-                    multiply_pass(*LAST_PAIR, half, 0)
+                    multiply_pass(g, pair, half, 0)
             for half in range(2):
-                multiply_pass(*LAST_PAIR, half, c)
+                multiply_pass(g, pair, half, c)
 
         def activate(g, pair):
             if g == 0:
@@ -291,7 +293,7 @@ def tile_lstm_pa_kernel(tc, x, Wxi, bxi, Wxc, bxc, Wxo, bxo, out):
         bias_cols = None
         complete = []
         started = [[], [], []]
-        last_pair_pass = 0
+        early_passes = []
         begun = 0
         finished = 0
         step = 0
@@ -303,9 +305,9 @@ def tile_lstm_pa_kernel(tc, x, Wxi, bxi, Wxc, bxc, Wxo, bxo, out):
             started.append(batch)
             for pair in batch:
                 multiply(*pair)
-            if last_pair_pass:
-                multiply_last_pair(last_pair_pass)
-                last_pair_pass = 0
+            for pair, c in early_passes:
+                multiply_early(pair, c)
+            early_passes = []
             if 0 <= x_first_step + PASSES - step < WARM_STEPS:
                 warm_bank = turn_psum.tile([P, WARM_COLS], F32, tag="turned")
                 for repeat in range(WARM_MATMULS):
@@ -350,8 +352,14 @@ def tile_lstm_pa_kernel(tc, x, Wxi, bxi, Wxc, bxc, Wxo, bxo, out):
                     complete.extend(
                         [(g, pair) for pair in range(first // PAIR, (first + width) // PAIR)]
                     )
-                elif (g, first // PAIR) == LAST_PAIR and c > 0:
-                    last_pair_pass = c
+                elif g == GATES - 1 and c > 0:
+                    early_passes.extend(
+                        [
+                            (pair, c)
+                            for pair in range(first // PAIR, (first + width) // PAIR)
+                            if pair in EARLY
+                        ]
+                    )
             if step == x_first_step + PASSES:
                 bias_cols = turn_biases(nc, const, turn_psum, identity, bias_rows)
             if 0 <= step - x_first_step < PASSES:

@@ -23,39 +23,33 @@ N_TILES = D_OUT // P
 PAIR = 2 * P
 PAIRS = D_OUT // PAIR
 LAST_PAIR = (GATES - 1, PAIRS - 1)
-EARLY = [5, 6, 7]
+RANGES = [[512, 512, 1024], [1024, 1024], [1024, 512, 256, 256]]
 
 SLICE = 512
 
-BASE_COLS = 248
+BASE_COLS = 160
 PASS_COLS = 88
+PE_COLS = 256
+COL_STEP = 8
 PAIR_VECTOR_COLS = 168
 
-WARM_STEPS = 2
-WARM_COLS = 512
-WARM_MATMULS = 2
-
-RAW_BUFS = 5
+RAW_BUFS = 10
 QUANTISE_LAG = 2
-FIRST_PART = SLICE
-FIRST_PASSES = 8
-PART = 2 * SLICE
-X_BEHIND = 5
+X_LOAD_BEHIND = 2
+X_STEP = 3
+BACKLOG = 8
 
 FLOPS = 2 * B * D_IN * D_OUT * GATES
 
 
-def unit_order():
-    units = []
+def range_order():
+    ranges = []
     for g in range(GATES):
-        by_pass = PASSES if g < GATES - 1 else 1
-        for c in range(by_pass):
-            units.extend([(g, c, first, SLICE) for first in range(0, D_OUT, SLICE)])
-        for first in range(0, D_OUT - SLICE, SLICE):
-            units.extend([(g, c, first, SLICE) for c in range(by_pass, PASSES)])
-        for first in range(D_OUT - SLICE, D_OUT, PAIR):
-            units.extend([(g, c, first, PAIR) for c in range(by_pass, PASSES)])
-    return units
+        first = 0
+        for width in RANGES[g]:
+            ranges.append((g, first, width))
+            first += width
+    return ranges
 
 
 def load_biases(nc, bias_rows, biases):
@@ -66,14 +60,12 @@ def load_biases(nc, bias_rows, biases):
         )
 
 
-def turn_biases(nc, const, turn_psum, identity, bias_rows):
+def spread_biases(nc, const, turn_psum, identity, bias_rows):
     bias_rows_f32 = const.tile([P, P], F32)
     nc.vector.tensor_copy(out=bias_rows_f32[:], in_=bias_rows[:])
     bias_turned = turn_psum.tile([P, P], F32, tag="turned")
     nc.tensor.transpose(bias_turned[:], bias_rows_f32[:], identity[:])
-    bias_cols = const.tile([P, P], F32)
-    nc.vector.tensor_copy(out=bias_cols[:], in_=bias_turned[:])
-    return bias_cols
+    return bias_turned
 
 
 def turn_x(nc, x_pool, turn_psum, identity, x_rows, c):
@@ -94,16 +86,35 @@ def turn_x(nc, x_pool, turn_psum, identity, x_rows, c):
     return x_grouped
 
 
-def regroup(nc, grouped_pool, raw_cols, width, vector_cols):
+def regroup_on_tensor(nc, turn_psum, identity_bf16, raw_cols):
+    bank = turn_psum.tile([P, PE_COLS, PACK], BF16, tag="turned")
+    for first in range(0, PE_COLS, P):
+        nc.tensor.matmul(
+            out=bank[:, first : first + P, :].rearrange("p w j -> p j w"),
+            lhsT=identity_bf16[:],
+            rhs=raw_cols[:, :, first : first + P],
+            start=True,
+            stop=True,
+        )
+    return bank
+
+
+def regroup(nc, grouped_pool, raw_cols, width, vector_cols, bank):
     grouped = grouped_pool.tile([P, width, PACK], BF16, tag="grouped", align_bytes=64)
     nc.vector.tensor_copy(
         out=grouped[:, :vector_cols, :].rearrange("p (r i) j -> p r j i", i=4),
         in_=raw_cols[:, :, :vector_cols].rearrange("p j (r i) -> p r j i", i=4),
     )
-    nc.scalar.copy(
-        out=grouped[:, vector_cols:, :].rearrange("p (r i) j -> p r j i", i=4),
-        in_=raw_cols[:, :, vector_cols:].rearrange("p j (r i) -> p r j i", i=4),
-    )
+    if bank is None:
+        nc.scalar.copy(
+            out=grouped[:, vector_cols:, :].rearrange("p (r i) j -> p r j i", i=4),
+            in_=raw_cols[:, :, vector_cols:].rearrange("p j (r i) -> p r j i", i=4),
+        )
+    else:
+        nc.scalar.copy(
+            out=grouped[:, vector_cols:, :].rearrange("p w j -> p (w j)").bitcast(F32),
+            in_=bank.rearrange("p w j -> p (w j)").bitcast(F32),
+        )
     return grouped
 
 
@@ -131,9 +142,10 @@ def tile_lstm_pa_kernel(tc, x, Wxi, bxi, Wxc, bxc, Wxo, bxo, out):
         raw_pool = ctx.enter_context(tc.tile_pool(name="raw", bufs=RAW_BUFS))
         grouped_pool = ctx.enter_context(tc.tile_pool(name="grouped", bufs=QUANTISE_LAG + 2))
         x_pool = ctx.enter_context(tc.tile_pool(name="x_grouped", bufs=2))
-        quantised = ctx.enter_context(tc.tile_pool(name="quantised", bufs=2))
+        quantised = ctx.enter_context(tc.tile_pool(name="quantised", bufs=3))
         kept = ctx.enter_context(tc.tile_pool(name="kept", bufs=PAIRS))
         work = ctx.enter_context(tc.tile_pool(name="work", bufs=3))
+        results = ctx.enter_context(tc.tile_pool(name="results", bufs=PAIRS))
         acc_psum = ctx.enter_context(tc.psum_pool(name="acc", bufs=4))
         turn_psum = ctx.enter_context(tc.psum_pool(name="turn", bufs=4))
 
@@ -144,15 +156,23 @@ def tile_lstm_pa_kernel(tc, x, Wxi, bxi, Wxc, bxc, Wxo, bxo, out):
 
         identity = const.tile([P, P], F32)
         make_identity(nc, identity[:])
+        identity_bf16 = const.tile([P, P], BF16)
+        make_identity(nc, identity_bf16[:])
         x_codes = const.tile([P, PASSES, B], U32, align_bytes=64)
         x_scales = const.tile([P, PASSES, B], U8, align_bytes=64)
 
+        ranges = range_order()
         raws = {}
         codes = {}
         accs = {}
         gates = {}
         turned_banks = {}
         tanh_states = {}
+        range_of = {}
+
+        for r, (g, first, width) in enumerate(ranges):
+            for pair in range(first // PAIR, (first + width) // PAIR):
+                range_of[(g, pair)] = r
 
         def load_x(c):
             nc.sync.dma_start(
@@ -160,97 +180,68 @@ def tile_lstm_pa_kernel(tc, x, Wxi, bxi, Wxc, bxc, Wxo, bxo, out):
                 in_=x.rearrange("(a p) k -> p a k", p=P)[:, :, c * K_PASS : (c + 1) * K_PASS],
             )
 
-        def part_width(k):
-            return FIRST_PART if k < FIRST_PASSES else PART
-
-        def load_part(k, e):
-            g, c = divmod(k, PASSES)
-            width = part_width(k)
+        def load_pass(r, c):
+            g, first, width = ranges[r]
+            raw = raw_pool.tile([P, PACK, width], BF16, tag="raw")
+            raws[(r, c)] = raw
             nc.sync.dma_start(
-                out=raws[k][:, e, :, :],
-                in_=weights[g][
-                    c * K_PASS : (c + 1) * K_PASS, e * width : (e + 1) * width
-                ].rearrange("(p j) w -> p j w", j=PACK),
+                out=raw[:],
+                in_=weights[g][c * K_PASS : (c + 1) * K_PASS, first : first + width].rearrange(
+                    "(p j) w -> p j w", j=PACK
+                ),
             )
 
-        def load_pass(k):
-            parts = D_OUT // part_width(k)
-            raw = raw_pool.tile([P, parts, PACK, part_width(k)], BF16, tag="raw")
-            raws[k] = raw
-            by_columns = range((GATES - 1) * PASSES + 1, GATES * PASSES)
-            if k not in by_columns:
-                for e in range(parts):
-                    load_part(k, e)
-                    if k == X_BEHIND and e + 1 < PASSES:
-                        load_x(e + 1)
-                return
-            load_part(k, 0)
-            if k == by_columns[-1]:
-                for e in range(1, parts):
-                    for k_late in by_columns:
-                        load_part(k_late, e)
-
-        def unit_cols(g, c, first, width):
-            k = g * PASSES + c
-            inside = first % part_width(k)
-            return raws[k][:, first // part_width(k), :, inside : inside + width]
-
-        def quantise_unit(grouped, g, c, first, width):
-            w_codes, w_scales = codes[g]
+        def quantise_unit(grouped, r, c, inside, width):
+            w_codes, w_scales = codes[r]
             nc.vector.quantize_mx(
-                out=w_codes[:, c, first : first + width].bitcast(FP8X4),
-                scales=w_scales[:, c, first : first + width],
+                out=w_codes[:, c, inside : inside + width].bitcast(FP8X4),
+                scales=w_scales[:, c, inside : inside + width],
                 in_=grouped.rearrange("p w j -> p (w j)"),
             )
 
         def multiply_pass(g, pair, half, c):
-            w_codes, w_scales = codes[g]
-            t = 2 * pair + half
+            r = range_of[(g, pair)]
+            w_codes, w_scales = codes[r]
+            at = pair * PAIR + half * P - ranges[r][1]
             nc.tensor.matmul_mx(
-                out=accs[(g, pair)][half],
-                lhsT=w_codes[:, c, t * P : (t + 1) * P].bitcast(FP8X4),
-                lhsT_scale=w_scales[:, c, t * P : (t + 1) * P],
+                out=accs[(g, pair, half)],
+                lhsT=w_codes[:, c, at : at + P].bitcast(FP8X4),
+                lhsT_scale=w_scales[:, c, at : at + P],
                 rhs=x_codes[:, c, :].bitcast(FP8X4),
                 rhs_scale=x_scales[:, c, :],
                 start=(c == 0),
                 stop=(c == PASSES - 1),
             )
 
-        def multiply(g, pair):
-            if g == GATES - 1 and pair in EARLY:
-                multiply_early(pair, PASSES - 1)
-                return
-            acc = acc_psum.tile([P, 2, B], F32, tag="acc")
-            accs[(g, pair)] = [acc[:, half, :] for half in range(2)]
-            for half in range(2):
-                for c in range(PASSES):
-                    multiply_pass(g, pair, half, c)
+        def multiply(g, pair, half):
+            acc = acc_psum.tile([P, B], F32, tag="acc")
+            accs[(g, pair, half)] = acc[:]
+            for c in range(PASSES):
+                multiply_pass(g, pair, half, c)
 
-        def multiply_early(pair, c):
-            g = GATES - 1
-            if c == 1:
+        def multiply_early(g, pair, c):
+            if c == 0:
                 acc_0 = acc_psum.tile([P, B], F32, tag="acc")
                 acc_1 = acc_psum.tile([P, B], F32, tag="acc")
-                accs[(g, pair)] = [acc_0[:], acc_1[:]]
-                for half in range(2):
-                    multiply_pass(g, pair, half, 0)
+                accs[(g, pair, 0)] = acc_0[:]
+                accs[(g, pair, 1)] = acc_1[:]
             for half in range(2):
                 multiply_pass(g, pair, half, c)
 
-        def activate(g, pair):
-            if g == 0:
-                gate = kept.tile([P, 2, B], F32, tag="kept")
-            else:
-                gate = work.tile([P, 2, B], F32, tag="gate")
-            for half in range(2):
-                t = 2 * pair + half
-                nc.scalar.activation(
-                    out=gate[:, half, :],
-                    in_=accs[(g, pair)][half],
-                    func=functions[g],
-                    bias=bias_cols[:, g * N_TILES + t : g * N_TILES + t + 1],
-                )
-            gates[(g, pair)] = gate
+        def activate(g, pair, half):
+            if half == 0:
+                if g == 0:
+                    gate = kept.tile([P, 2, B], F32, tag="kept")
+                else:
+                    gate = work.tile([P, 2, B], F32, tag="gate")
+                gates[(g, pair)] = gate
+            t = 2 * pair + half
+            nc.scalar.activation(
+                out=gates[(g, pair)][:, half, :],
+                in_=accs[(g, pair, half)],
+                func=functions[g],
+                bias=bias_cols[:, g * N_TILES + t : g * N_TILES + t + 1],
+            )
 
         def combine(g, pair):
             if g == 1:
@@ -270,7 +261,7 @@ def tile_lstm_pa_kernel(tc, x, Wxi, bxi, Wxc, bxc, Wxo, bxo, out):
                 )
                 tanh_states[pair] = tanh_state
             if g == 2:
-                result = work.tile([P, M_TILES, PAIR], F32, tag="result")
+                result = results.tile([P, M_TILES, PAIR], F32, tag="result")
                 nc.vector.tensor_mul(
                     out=result[:], in0=turned_banks[(g, pair)][:], in1=tanh_states[pair][:]
                 )
@@ -282,101 +273,123 @@ def tile_lstm_pa_kernel(tc, x, Wxi, bxi, Wxc, bxc, Wxo, bxo, out):
         nc.vector.memset(bias_rows[:].bitcast(I32), 0)
         load_biases(nc, bias_rows, [bxi, bxc, bxo])
         x_rows = const.tile([P, M_TILES * D_IN], BF16)
-        for k in range(RAW_BUFS):
-            load_pass(k)
-        load_x(0)
 
-        units = unit_order()
-        x_first_step = units.index((X_BEHIND // PASSES, X_BEHIND % PASSES, 0, SLICE))
+        loads = [(r, c) for r in range(len(ranges)) for c in range(PASSES)]
+        units = []
+        for r, (g, first, width) in enumerate(ranges):
+            for c in range(PASSES):
+                for inside in range(0, width, SLICE):
+                    units.append((r, c, inside, min(SLICE, width)))
+        for at in range(RAW_BUFS):
+            load_pass(*loads[at])
+            if X_LOAD_BEHIND <= at < X_LOAD_BEHIND + PASSES:
+                load_x(at - X_LOAD_BEHIND)
+
+        banks = {}
+        net_before = 0
         regrouped = {}
         x_grouped = {}
-        bias_cols = None
-        complete = []
-        started = [[], [], []]
+        bias_turned = None
+        bias_cols = const.tile([P, P], F32)
+        waiting = []
         early_passes = []
-        begun = 0
+        to_activate = []
+        to_combine = []
+        to_finish = []
         finished = 0
         step = 0
         while finished < GATES * PAIRS:
-            batch = []
-            if step > x_first_step + PASSES:
-                batch = complete[begun : begun + 1]
-            begun += len(batch)
-            started.append(batch)
-            for pair in batch:
-                multiply(*pair)
-            for pair, c in early_passes:
-                multiply_early(pair, c)
-            early_passes = []
-            if 0 <= x_first_step + PASSES - step < WARM_STEPS:
-                warm_bank = turn_psum.tile([P, WARM_COLS], F32, tag="turned")
-                for repeat in range(WARM_MATMULS):
-                    nc.tensor.matmul(
-                        out=warm_bank[:],
-                        lhsT=x_rows[:, :P],
-                        rhs=x_rows[:, :WARM_COLS],
-                        start=True,
-                        stop=True,
-                    )
-            if step < len(units):
-                g, c, first, width = units[step]
-                if c == 0 and first == 0:
-                    w_codes = quantised.tile([P, PASSES, D_OUT], U32, align_bytes=64)
-                    w_scales = quantised.tile([P, PASSES, D_OUT], U8, align_bytes=64)
-                    codes[g] = (w_codes, w_scales)
-                scalar_passes = (
-                    len(started[-2])
-                    + len([pair for pair in started[-4] if pair[0] == 1])
-                    + (0 <= step - x_first_step < PASSES)
-                )
-                vector_passes = len([pair for pair in started[-3] if pair[0] == 1]) + len(
-                    [pair for pair in started[-4] if pair[0] == 2]
-                )
-                vector_cols = BASE_COLS + PASS_COLS * (scalar_passes - vector_passes)
-                if width == PAIR:
-                    vector_cols = PAIR_VECTOR_COLS
-                regrouped[step] = regroup(
-                    nc,
-                    grouped_pool,
-                    unit_cols(g, c, first, width),
-                    width,
-                    vector_cols,
-                )
-                next_load = g * PASSES + c + RAW_BUFS
-                if first + width == D_OUT and next_load < GATES * PASSES:
-                    load_pass(next_load)
-            if QUANTISE_LAG <= step < len(units) + QUANTISE_LAG:
-                g, c, first, width = units[step - QUANTISE_LAG]
-                quantise_unit(regrouped[step - QUANTISE_LAG], g, c, first, width)
+            activating, combining, finishing = to_activate, to_combine, to_finish
+            to_activate, to_combine, to_finish = [], [], []
+            if step > X_STEP + PASSES:
+                count = 2 if len(waiting) > BACKLOG else 1
+                for item in waiting[:count]:
+                    multiply(*item)
+                    to_activate.append(item)
+                waiting = waiting[count:]
+            for g, pair, c in early_passes:
+                multiply_early(g, pair, c)
                 if c == PASSES - 1:
-                    complete.extend(
-                        [(g, pair) for pair in range(first // PAIR, (first + width) // PAIR)]
-                    )
-                elif g == GATES - 1 and c > 0:
-                    early_passes.extend(
-                        [
-                            (pair, c)
-                            for pair in range(first // PAIR, (first + width) // PAIR)
-                            if pair in EARLY
-                        ]
-                    )
-            if step == x_first_step + PASSES:
-                bias_cols = turn_biases(nc, const, turn_psum, identity, bias_rows)
-            if 0 <= step - x_first_step < PASSES:
-                c = step - x_first_step
+                    to_activate.extend([(g, pair, 0), (g, pair, 1)])
+            early_passes = []
+            if step == X_STEP + PASSES - 1:
+                bias_turned = spread_biases(nc, const, turn_psum, identity, bias_rows)
+            if step == X_STEP + PASSES:
+                nc.vector.tensor_copy(out=bias_cols[:], in_=bias_turned[:])
+            if 0 <= step - X_STEP < PASSES:
+                c = step - X_STEP
                 x_grouped[c] = turn_x(nc, x_pool, turn_psum, identity, x_rows, c)
-            if 0 <= step - x_first_step - 1 < PASSES:
-                c = step - x_first_step - 1
+            if 0 <= step - X_STEP - 1 < PASSES:
+                c = step - X_STEP - 1
                 nc.vector.quantize_mx(
                     out=x_codes[:, c, :].bitcast(FP8X4),
                     scales=x_scales[:, c, :],
                     in_=x_grouped[c][:],
                 )
-            for pair in started[-4]:
-                finish(*pair)
+            if X_STEP + PASSES <= step + 1 < len(units) and (step + 1) % 2 == 1 and units[step + 1][3] == SLICE:
+                r, c, inside, width = units[step + 1]
+                banks[step + 1] = regroup_on_tensor(
+                    nc,
+                    turn_psum,
+                    identity_bf16,
+                    raws[(r, c)][:, :, inside + width - PE_COLS : inside + width],
+                )
+            if 0 <= step < len(units):
+                r, c, inside, width = units[step]
+                if c == 0 and inside == 0:
+                    w_codes = quantised.tile([P, PASSES, ranges[r][2]], U32, align_bytes=64)
+                    w_scales = quantised.tile([P, PASSES, ranges[r][2]], U8, align_bytes=64)
+                    codes[r] = (w_codes, w_scales)
+                scalar_passes = (
+                    0.5 * len(activating)
+                    + len([pair for pair in finishing if pair[0] == 1])
+                    + (0 <= step - X_STEP < PASSES)
+                )
+                vector_passes = len([pair for pair in combining if pair[0] == 1]) + len(
+                    [pair for pair in finishing if pair[0] == 2]
+                )
+                net = scalar_passes - vector_passes
+                if step in banks:
+                    vector_cols = width - PE_COLS
+                else:
+                    vector_cols = COL_STEP * round(
+                        (BASE_COLS + PASS_COLS * (net + net_before)) / COL_STEP
+                    )
+                net_before = net if step in banks else 0
+                if width == PAIR:
+                    vector_cols = PAIR_VECTOR_COLS
+                regrouped[step] = regroup(
+                    nc,
+                    grouped_pool,
+                    raws[(r, c)][:, :, inside : inside + width],
+                    width,
+                    vector_cols,
+                    banks.get(step),
+                )
+                if inside + width == ranges[r][2]:
+                    at = r * PASSES + c + RAW_BUFS
+                    if at < len(loads):
+                        load_pass(*loads[at])
+            for g, pair in combining:
+                combine(g, pair)
+                to_finish.append((g, pair))
+            if QUANTISE_LAG <= step < len(units) + QUANTISE_LAG:
+                r, c, inside, width = units[step - QUANTISE_LAG]
+                quantise_unit(regrouped[step - QUANTISE_LAG], r, c, inside, width)
+                g, range_first, range_width = ranges[r]
+                pairs = range((range_first + inside) // PAIR, (range_first + inside + width) // PAIR)
+                if range_width == PAIR:
+                    early_passes.extend([(g, pair, c) for pair in pairs])
+                elif c == PASSES - 1:
+                    waiting.extend([(g, pair, half) for pair in pairs for half in range(2)])
+            for g, pair in finishing:
+                finish(g, pair)
                 finished += 1
-            for pair in started[-2]:
-                activate(*pair)
-            for pair in started[-3]:
-                combine(*pair)
+            for g, pair, half in activating:
+                activate(g, pair, half)
+                if half == 1:
+                    if g == 0:
+                        finished += 1
+                    else:
+                        to_combine.append((g, pair))
             step += 1

@@ -36,6 +36,7 @@ PAIR_VECTOR_COLS = 168
 RAW_BUFS = 10
 QUANTISE_LAG = 2
 X_LOAD_BEHIND = 2
+BIAS_STEP = 0
 X_STEP = 3
 BACKLOG = 8
 
@@ -102,13 +103,13 @@ def regroup_on_tensor(nc, turn_psum, identity_bf16, raw_cols):
 def regroup(nc, grouped_pool, raw_cols, width, vector_cols, bank):
     grouped = grouped_pool.tile([P, width, PACK], BF16, tag="grouped", align_bytes=64)
     nc.vector.tensor_copy(
-        out=grouped[:, :vector_cols, :].rearrange("p (r i) j -> p r j i", i=4),
-        in_=raw_cols[:, :, :vector_cols].rearrange("p j (r i) -> p r j i", i=4),
+        out=grouped[:, :vector_cols, :].rearrange("p (r i) j -> p r j i", i=2),
+        in_=raw_cols[:, :, :vector_cols].rearrange("p j (r i) -> p r j i", i=2),
     )
     if bank is None:
         nc.scalar.copy(
-            out=grouped[:, vector_cols:, :].rearrange("p (r i) j -> p r j i", i=4),
-            in_=raw_cols[:, :, vector_cols:].rearrange("p j (r i) -> p r j i", i=4),
+            out=grouped[:, vector_cols:, :].rearrange("p (r i) j -> p r j i", i=2),
+            in_=raw_cols[:, :, vector_cols:].rearrange("p j (r i) -> p r j i", i=2),
         )
     else:
         nc.scalar.copy(
@@ -166,6 +167,7 @@ def tile_lstm_pa_kernel(tc, x, Wxi, bxi, Wxc, bxc, Wxo, bxo, out):
         codes = {}
         accs = {}
         gates = {}
+        states = {}
         turned_banks = {}
         tanh_states = {}
         range_of = {}
@@ -243,15 +245,16 @@ def tile_lstm_pa_kernel(tc, x, Wxi, bxi, Wxc, bxc, Wxo, bxo, out):
                 bias=bias_cols[:, g * N_TILES + t : g * N_TILES + t + 1],
             )
 
-        def combine(g, pair):
-            if g == 1:
-                state = work.tile([P, 2, B], F32, tag="state")
-                nc.vector.tensor_mul(
-                    out=state[:], in0=gates[(1, pair)][:], in1=gates[(0, pair)][:]
-                )
-                turned_banks[(g, pair)] = turn_pair(nc, turn_psum, identity, state)
-            if g == 2:
-                turned_banks[(g, pair)] = turn_pair(nc, turn_psum, identity, gates[(2, pair)])
+        def combine(pair):
+            state = work.tile([P, 2, B], F32, tag="state")
+            nc.vector.tensor_mul(
+                out=state[:], in0=gates[(1, pair)][:], in1=gates[(0, pair)][:]
+            )
+            states[pair] = state
+
+        def turn(g, pair):
+            values = states[pair] if g == 1 else gates[(2, pair)]
+            turned_banks[(g, pair)] = turn_pair(nc, turn_psum, identity, values)
 
         def finish(g, pair):
             if g == 1:
@@ -295,12 +298,13 @@ def tile_lstm_pa_kernel(tc, x, Wxi, bxi, Wxc, bxc, Wxo, bxo, out):
         early_passes = []
         to_activate = []
         to_combine = []
+        to_turn = []
         to_finish = []
         finished = 0
         step = 0
         while finished < GATES * PAIRS:
-            activating, combining, finishing = to_activate, to_combine, to_finish
-            to_activate, to_combine, to_finish = [], [], []
+            activating, combining, turning, finishing = to_activate, to_combine, to_turn, to_finish
+            to_activate, to_combine, to_turn, to_finish = [], [], [], []
             if step > X_STEP + PASSES:
                 count = 2 if len(waiting) > BACKLOG else 1
                 for item in waiting[:count]:
@@ -312,9 +316,12 @@ def tile_lstm_pa_kernel(tc, x, Wxi, bxi, Wxc, bxc, Wxo, bxo, out):
                 if c == PASSES - 1:
                     to_activate.extend([(g, pair, 0), (g, pair, 1)])
             early_passes = []
-            if step == X_STEP + PASSES - 1:
+            for g, pair in turning:
+                turn(g, pair)
+                to_finish.append((g, pair))
+            if step == BIAS_STEP:
                 bias_turned = spread_biases(nc, const, turn_psum, identity, bias_rows)
-            if step == X_STEP + PASSES:
+            if step == BIAS_STEP + 1:
                 nc.vector.tensor_copy(out=bias_cols[:], in_=bias_turned[:])
             if 0 <= step - X_STEP < PASSES:
                 c = step - X_STEP
@@ -345,15 +352,16 @@ def tile_lstm_pa_kernel(tc, x, Wxi, bxi, Wxc, bxc, Wxo, bxo, out):
                     + len([pair for pair in finishing if pair[0] == 1])
                     + (0 <= step - X_STEP < PASSES)
                 )
-                vector_passes = len([pair for pair in combining if pair[0] == 1]) + len(
+                vector_passes = len(combining) + len(
                     [pair for pair in finishing if pair[0] == 2]
                 )
                 net = scalar_passes - vector_passes
                 if step in banks:
                     vector_cols = width - PE_COLS
                 else:
+                    base = BASE_COLS if step >= X_STEP + PASSES else 232
                     vector_cols = COL_STEP * round(
-                        (BASE_COLS + PASS_COLS * (net + net_before)) / COL_STEP
+                        (base + PASS_COLS * (net + net_before)) / COL_STEP
                     )
                 net_before = net if step in banks else 0
                 if width == PAIR:
@@ -370,9 +378,9 @@ def tile_lstm_pa_kernel(tc, x, Wxi, bxi, Wxc, bxc, Wxo, bxo, out):
                     at = r * PASSES + c + RAW_BUFS
                     if at < len(loads):
                         load_pass(*loads[at])
-            for g, pair in combining:
-                combine(g, pair)
-                to_finish.append((g, pair))
+            for pair in combining:
+                combine(pair)
+                to_turn.append((1, pair))
             if QUANTISE_LAG <= step < len(units) + QUANTISE_LAG:
                 r, c, inside, width = units[step - QUANTISE_LAG]
                 quantise_unit(regrouped[step - QUANTISE_LAG], r, c, inside, width)
@@ -390,6 +398,8 @@ def tile_lstm_pa_kernel(tc, x, Wxi, bxi, Wxc, bxc, Wxo, bxo, out):
                 if half == 1:
                     if g == 0:
                         finished += 1
+                    elif g == 1:
+                        to_combine.append(pair)
                     else:
-                        to_combine.append((g, pair))
+                        to_turn.append((g, pair))
             step += 1

@@ -316,6 +316,8 @@ def tile_lstm_pa_kernel(tc, x, Wxi, bxi, Wxc, bxc, Wxo, bxo, out):
                 if c == PASSES - 1:
                     to_activate.extend([(g, pair, 0), (g, pair, 1)])
             early_passes = []
+            if len(turning) == 1 and step < len(units) - 4:
+                to_turn, turning = turning, []
             for g, pair in turning:
                 turn(g, pair)
                 to_finish.append((g, pair))

@@ -23,7 +23,7 @@ N_TILES = D_OUT // P
 PAIR = 2 * P
 PAIRS = D_OUT // PAIR
 LAST_PAIR = (GATES - 1, PAIRS - 1)
-RANGES = [[512, 512, 1024], [1024, 1024], [1024, 512, 256, 256]]
+RANGES = [[512, 512, 512, 512], [512, 512, 512, 512], [512, 512, 512, 256, 256]]
 
 SLICE = 512
 
@@ -33,11 +33,10 @@ PE_COLS = 256
 COL_STEP = 8
 PAIR_VECTOR_COLS = 168
 
-RAW_BUFS = 10
-QUANTISE_LAG = 2
-X_LOAD_BEHIND = 2
-BIAS_STEP = 0
-X_STEP = 3
+RAW_BUFS = 18
+QUANTISE_LAG = 1
+BIAS_STEP = 1
+X_STEP = -4
 BACKLOG = 8
 
 FLOPS = 2 * B * D_IN * D_OUT * GATES
@@ -142,13 +141,17 @@ def tile_lstm_pa_kernel(tc, x, Wxi, bxi, Wxc, bxc, Wxo, bxo, out):
         const = ctx.enter_context(tc.tile_pool(name="const", bufs=1))
         raw_pool = ctx.enter_context(tc.tile_pool(name="raw", bufs=RAW_BUFS))
         grouped_pool = ctx.enter_context(tc.tile_pool(name="grouped", bufs=QUANTISE_LAG + 2))
-        x_pool = ctx.enter_context(tc.tile_pool(name="x_grouped", bufs=2))
+        x_pool = ctx.enter_context(tc.tile_pool(name="x_grouped", bufs=4))
         quantised = ctx.enter_context(tc.tile_pool(name="quantised", bufs=3))
         kept = ctx.enter_context(tc.tile_pool(name="kept", bufs=PAIRS))
         work = ctx.enter_context(tc.tile_pool(name="work", bufs=3))
         results = ctx.enter_context(tc.tile_pool(name="results", bufs=PAIRS))
         acc_psum = ctx.enter_context(tc.psum_pool(name="acc", bufs=4))
         turn_psum = ctx.enter_context(tc.psum_pool(name="turn", bufs=4))
+
+        bias_rows = const.tile([P, P], BF16)
+        nc.vector.memset(bias_rows[:].bitcast(I32), 0)
+        load_biases(nc, bias_rows, [bxi, bxc, bxo])
 
         table_in = const.tile([P, 1], F32)
         table_out = const.tile([P, 1], F32)
@@ -272,9 +275,6 @@ def tile_lstm_pa_kernel(tc, x, Wxi, bxi, Wxc, bxc, Wxo, bxo, out):
                     out=out_view[:, :, pair * PAIR : (pair + 1) * PAIR], in_=result[:]
                 )
 
-        bias_rows = const.tile([P, P], BF16)
-        nc.vector.memset(bias_rows[:].bitcast(I32), 0)
-        load_biases(nc, bias_rows, [bxi, bxc, bxo])
         x_rows = const.tile([P, M_TILES * D_IN], BF16)
 
         loads = [(r, c) for r in range(len(ranges)) for c in range(PASSES)]
@@ -283,10 +283,10 @@ def tile_lstm_pa_kernel(tc, x, Wxi, bxi, Wxc, bxc, Wxo, bxo, out):
             for c in range(PASSES):
                 for inside in range(0, width, SLICE):
                     units.append((r, c, inside, min(SLICE, width)))
+        for c in range(PASSES):
+            load_x(c)
         for at in range(RAW_BUFS):
             load_pass(*loads[at])
-            if X_LOAD_BEHIND <= at < X_LOAD_BEHIND + PASSES:
-                load_x(at - X_LOAD_BEHIND)
 
         banks = {}
         net_before = 0
@@ -299,12 +299,18 @@ def tile_lstm_pa_kernel(tc, x, Wxi, bxi, Wxc, bxc, Wxo, bxo, out):
         to_activate = []
         to_combine = []
         to_turn = []
+        held = []
         to_finish = []
         finished = 0
-        step = 0
+        step = X_STEP
         while finished < GATES * PAIRS:
             activating, combining, turning, finishing = to_activate, to_combine, to_turn, to_finish
             to_activate, to_combine, to_turn, to_finish = [], [], [], []
+            if step < len(units):
+                held, combining = combining, held
+            else:
+                combining = held + combining
+                held = []
             if step > X_STEP + PASSES:
                 count = 2 if len(waiting) > BACKLOG else 1
                 for item in waiting[:count]:
@@ -316,7 +322,7 @@ def tile_lstm_pa_kernel(tc, x, Wxi, bxi, Wxc, bxc, Wxo, bxo, out):
                 if c == PASSES - 1:
                     to_activate.extend([(g, pair, 0), (g, pair, 1)])
             early_passes = []
-            if len(turning) == 1 and step < len(units) - 4:
+            if len(turning) == 1 and step < len(units) - 1:
                 to_turn, turning = turning, []
             for g, pair in turning:
                 turn(g, pair)
@@ -335,7 +341,7 @@ def tile_lstm_pa_kernel(tc, x, Wxi, bxi, Wxc, bxc, Wxo, bxo, out):
                     scales=x_scales[:, c, :],
                     in_=x_grouped[c][:],
                 )
-            if X_STEP + PASSES <= step + 1 < len(units) and (step + 1) % 2 == 1 and units[step + 1][3] == SLICE:
+            if 7 <= step + 1 < len(units) and (step + 1) % 2 == 1 and units[step + 1][3] == SLICE:
                 r, c, inside, width = units[step + 1]
                 banks[step + 1] = regroup_on_tensor(
                     nc,
@@ -361,7 +367,7 @@ def tile_lstm_pa_kernel(tc, x, Wxi, bxi, Wxc, bxc, Wxo, bxo, out):
                 if step in banks:
                     vector_cols = width - PE_COLS
                 else:
-                    base = BASE_COLS if step >= X_STEP + PASSES else 232
+                    base = BASE_COLS if step >= 7 else 232
                     vector_cols = COL_STEP * round(
                         (base + PASS_COLS * (net + net_before)) / COL_STEP
                     )

from contextlib import ExitStack

import concourse.mybir as mybir
from concourse.masks import make_identity

F32 = mybir.dt.float32
BF16 = mybir.dt.bfloat16
I32 = mybir.dt.int32
U32 = mybir.dt.uint32
U8 = mybir.dt.uint8
FP8X4 = mybir.dt.float8_e4m3fn_x4
ACT = mybir.ActivationFunctionType

P = 128
PACK = 4
K_PASS = P * PACK

B, D_IN, D_OUT = 256, 2048, 2048
GATES = 3
PASSES = D_IN // K_PASS
M_TILES = B // P
N_TILES = D_OUT // P
PAIR = 2 * P
PAIRS = D_OUT // PAIR
LAST_PAIR = (GATES - 1, PAIRS - 1)
RANGES = [[512, 512, 512, 512], [512, 512, 512, 512], [512, 512, 512, 256, 256]]

SLICE = 512

BASE_COLS = 160
PASS_COLS = 88
PE_COLS = 256
COL_STEP = 8
PAIR_VECTOR_COLS = 168

RAW_BUFS = 18
QUANTISE_LAG = 1
BIAS_STEP = 1
X_STEP = -4
BACKLOG = 8

FLOPS = 2 * B * D_IN * D_OUT * GATES


def range_order():
    ranges = []
    for g in range(GATES):
        first = 0
        for width in RANGES[g]:
            ranges.append((g, first, width))
            first += width
    return ranges


def load_biases(nc, bias_rows, biases):
    for g in range(GATES):
        nc.scalar.dma_start(
            out=bias_rows[g * N_TILES : (g + 1) * N_TILES, :],
            in_=biases[g].rearrange("(t n) -> t n", n=P),
        )


def spread_biases(nc, const, turn_psum, identity, bias_rows):
    bias_rows_f32 = const.tile([P, P], F32)
    nc.vector.tensor_copy(out=bias_rows_f32[:], in_=bias_rows[:])
    bias_turned = turn_psum.tile([P, P], F32, tag="turned")
    nc.tensor.transpose(bias_turned[:], bias_rows_f32[:], identity[:])
    return bias_turned


def turn_x(nc, x_pool, turn_psum, identity, x_rows, c):
    x_words = x_rows[:].bitcast(F32).rearrange(
        "p (c a q u) -> p a c u q", a=M_TILES, c=PASSES, q=P, u=2
    )
    turned = turn_psum.tile([P, 2, B], F32, tag="turned")
    for u in range(2):
        for a in range(M_TILES):
            nc.tensor.transpose(
                turned[:, u, a * P : (a + 1) * P], x_words[:, a, c, u, :], identity[:]
            )
    x_grouped = x_pool.tile([P, B * PACK], BF16, tag="x_grouped", align_bytes=64)
    nc.scalar.copy(
        out=x_grouped[:].bitcast(F32).rearrange("p (m u) -> p m u", u=2),
        in_=turned.rearrange("p u m -> p m u"),
    )
    return x_grouped


def regroup_on_tensor(nc, turn_psum, identity_bf16, raw_cols):
    bank = turn_psum.tile([P, PE_COLS, PACK], BF16, tag="turned")
    for first in range(0, PE_COLS, P):
        nc.tensor.matmul(
            out=bank[:, first : first + P, :].rearrange("p w j -> p j w"),
            lhsT=identity_bf16[:],
            rhs=raw_cols[:, :, first : first + P],
            start=True,
            stop=True,
        )
    return bank


def regroup(nc, grouped_pool, raw_cols, width, vector_cols, bank):
    grouped = grouped_pool.tile([P, width, PACK], BF16, tag="grouped", align_bytes=64)
    nc.vector.tensor_copy(
        out=grouped[:, :vector_cols, :].rearrange("p (r i) j -> p r j i", i=2),
        in_=raw_cols[:, :, :vector_cols].rearrange("p j (r i) -> p r j i", i=2),
    )
    if bank is None:
        nc.scalar.copy(
            out=grouped[:, vector_cols:, :].rearrange("p (r i) j -> p r j i", i=2),
            in_=raw_cols[:, :, vector_cols:].rearrange("p j (r i) -> p r j i", i=2),
        )
    else:
        nc.scalar.copy(
            out=grouped[:, vector_cols:, :].rearrange("p w j -> p (w j)").bitcast(F32),
            in_=bank.rearrange("p w j -> p (w j)").bitcast(F32),
        )
    return grouped


def turn_pair(nc, turn_psum, identity, values):
    bank = turn_psum.tile([P, M_TILES, PAIR], F32, tag="turned")
    for half in range(2):
        for a in range(M_TILES):
            nc.tensor.transpose(
                bank[:, a, half * P : (half + 1) * P],
                values[:, half, a * P : (a + 1) * P],
                identity[:],
            )
    return bank


def tile_lstm_pa_kernel(tc, x, Wxi, bxi, Wxc, bxc, Wxo, bxo, out):
    nc = tc.nc
    weights = [Wxi, Wxc, Wxo]
    functions = [ACT.Sigmoid, ACT.Tanh, ACT.Sigmoid]
    out_view = out.rearrange("(a p) n -> p a n", p=P)

    with ExitStack() as ctx:
        ctx.enter_context(tc.manual_schedule())
        const = ctx.enter_context(tc.tile_pool(name="const", bufs=1))
        raw_pool = ctx.enter_context(tc.tile_pool(name="raw", bufs=RAW_BUFS))
        grouped_pool = ctx.enter_context(tc.tile_pool(name="grouped", bufs=QUANTISE_LAG + 2))
        x_pool = ctx.enter_context(tc.tile_pool(name="x_grouped", bufs=4))
        quantised = ctx.enter_context(tc.tile_pool(name="quantised", bufs=3))
        kept = ctx.enter_context(tc.tile_pool(name="kept", bufs=PAIRS))
        work = ctx.enter_context(tc.tile_pool(name="work", bufs=3))
        results = ctx.enter_context(tc.tile_pool(name="results", bufs=PAIRS))
        acc_psum = ctx.enter_context(tc.psum_pool(name="acc", bufs=4))
        turn_psum = ctx.enter_context(tc.psum_pool(name="turn", bufs=4))

        bias_rows = const.tile([P, P], BF16)
        nc.vector.memset(bias_rows[:].bitcast(I32), 0)
        load_biases(nc, bias_rows, [bxi, bxc, bxo])

        table_in = const.tile([P, 1], F32)
        table_out = const.tile([P, 1], F32)
        nc.vector.memset(table_in[:], 0.0)
        nc.scalar.activation(out=table_out[:], in_=table_in[:], func=ACT.Sigmoid)

        identity = const.tile([P, P], F32)
        make_identity(nc, identity[:])
        identity_bf16 = const.tile([P, P], BF16)
        make_identity(nc, identity_bf16[:])
        x_codes = const.tile([P, PASSES, B], U32, align_bytes=64)
        x_scales = const.tile([P, PASSES, B], U8, align_bytes=64)

        ranges = range_order()
        raws = {}
        codes = {}
        accs = {}
        gates = {}
        states = {}
        turned_banks = {}
        tanh_states = {}
        range_of = {}

        for r, (g, first, width) in enumerate(ranges):
            for pair in range(first // PAIR, (first + width) // PAIR):
                range_of[(g, pair)] = r

        def load_x(c):
            nc.sync.dma_start(
                out=x_rows.rearrange("p (c a k) -> p c a k", c=PASSES, a=M_TILES)[:, c, :, :],
                in_=x.rearrange("(a p) k -> p a k", p=P)[:, :, c * K_PASS : (c + 1) * K_PASS],
            )

        def load_pass(r, c):
            g, first, width = ranges[r]
            raw = raw_pool.tile([P, PACK, width], BF16, tag="raw")
            raws[(r, c)] = raw
            nc.sync.dma_start(
                out=raw[:],
                in_=weights[g][c * K_PASS : (c + 1) * K_PASS, first : first + width].rearrange(
                    "(p j) w -> p j w", j=PACK
                ),
            )

        def quantise_unit(grouped, r, c, inside, width):
            w_codes, w_scales = codes[r]
            nc.vector.quantize_mx(
                out=w_codes[:, c, inside : inside + width].bitcast(FP8X4),
                scales=w_scales[:, c, inside : inside + width],
                in_=grouped.rearrange("p w j -> p (w j)"),
            )

        def multiply_pass(g, pair, half, c):
            r = range_of[(g, pair)]
            w_codes, w_scales = codes[r]
            at = pair * PAIR + half * P - ranges[r][1]
            nc.tensor.matmul_mx(
                out=accs[(g, pair, half)],
                lhsT=w_codes[:, c, at : at + P].bitcast(FP8X4),
                lhsT_scale=w_scales[:, c, at : at + P],
                rhs=x_codes[:, c, :].bitcast(FP8X4),
                rhs_scale=x_scales[:, c, :],
                start=(c == 0),
                stop=(c == PASSES - 1),
            )

        def multiply(g, pair, half):
            acc = acc_psum.tile([P, B], F32, tag="acc")
            accs[(g, pair, half)] = acc[:]
            for c in range(PASSES):
                multiply_pass(g, pair, half, c)

        def multiply_early(g, pair, c):
            if c == 0:
                acc_0 = acc_psum.tile([P, B], F32, tag="acc")
                acc_1 = acc_psum.tile([P, B], F32, tag="acc")
                accs[(g, pair, 0)] = acc_0[:]
                accs[(g, pair, 1)] = acc_1[:]
            for half in range(2):
                multiply_pass(g, pair, half, c)

        def activate(g, pair, half):
            if half == 0:
                if g == 0:
                    gate = kept.tile([P, 2, B], F32, tag="kept")
                else:
                    gate = work.tile([P, 2, B], F32, tag="gate")
                gates[(g, pair)] = gate
            t = 2 * pair + half
            nc.scalar.activation(
                out=gates[(g, pair)][:, half, :],
                in_=accs[(g, pair, half)],
                func=functions[g],
                bias=bias_cols[:, g * N_TILES + t : g * N_TILES + t + 1],
            )

        def combine(pair):
            state = work.tile([P, 2, B], F32, tag="state")
            nc.vector.tensor_mul(
                out=state[:], in0=gates[(1, pair)][:], in1=gates[(0, pair)][:]
            )
            states[pair] = state

        def turn(g, pair):
            values = states[pair] if g == 1 else gates[(2, pair)]
            turned_banks[(g, pair)] = turn_pair(nc, turn_psum, identity, values)

        def finish(g, pair):
            if g == 1:
                tanh_state = kept.tile([P, M_TILES, PAIR], F32, tag="kept")
                nc.scalar.activation(
                    out=tanh_state[:], in_=turned_banks[(g, pair)][:], func=ACT.Tanh
                )
                tanh_states[pair] = tanh_state
            if g == 2:
                result = results.tile([P, M_TILES, PAIR], F32, tag="result")
                nc.vector.tensor_mul(
                    out=result[:], in0=turned_banks[(g, pair)][:], in1=tanh_states[pair][:]
                )
                nc.sync.dma_start(
                    out=out_view[:, :, pair * PAIR : (pair + 1) * PAIR], in_=result[:]
                )

        x_rows = const.tile([P, M_TILES * D_IN], BF16)

        loads = [(r, c) for r in range(len(ranges)) for c in range(PASSES)]
        units = []
        for r, (g, first, width) in enumerate(ranges):
            for c in range(PASSES):
                for inside in range(0, width, SLICE):
                    units.append((r, c, inside, min(SLICE, width)))
        for c in range(PASSES):
            load_x(c)
        for at in range(RAW_BUFS):
            load_pass(*loads[at])

        banks = {}
        net_before = 0
        regrouped = {}
        x_grouped = {}
        bias_turned = None
        bias_cols = const.tile([P, P], F32)
        waiting = []
        early_passes = []
        to_activate = []
        to_combine = []
        to_turn = []
        held = []
        to_finish = []
        finished = 0
        step = X_STEP
        while finished < GATES * PAIRS:
            activating, combining, turning, finishing = to_activate, to_combine, to_turn, to_finish
            to_activate, to_combine, to_turn, to_finish = [], [], [], []
            if step < len(units):
                held, combining = combining, held
            else:
                combining = held + combining
                held = []
            if step > X_STEP + PASSES:
                count = 2 if len(waiting) > BACKLOG else 1
                for item in waiting[:count]:
                    multiply(*item)
                    to_activate.append(item)
                waiting = waiting[count:]
            for g, pair, c in early_passes:
                multiply_early(g, pair, c)
                if c == PASSES - 1:
                    to_activate.extend([(g, pair, 0), (g, pair, 1)])
            early_passes = []
            if len(turning) == 1 and step < len(units) - 1:
                to_turn, turning = turning, []
            for g, pair in turning:
                turn(g, pair)
                to_finish.append((g, pair))
            if step == BIAS_STEP:
                bias_turned = spread_biases(nc, const, turn_psum, identity, bias_rows)
            if step == BIAS_STEP + 1:
                nc.vector.tensor_copy(out=bias_cols[:], in_=bias_turned[:])
            if 0 <= step - X_STEP < PASSES:
                c = step - X_STEP
                x_grouped[c] = turn_x(nc, x_pool, turn_psum, identity, x_rows, c)
            if 0 <= step - X_STEP - 1 < PASSES:
                c = step - X_STEP - 1
                nc.vector.quantize_mx(
                    out=x_codes[:, c, :].bitcast(FP8X4),
                    scales=x_scales[:, c, :],
                    in_=x_grouped[c][:],
                )
            if 7 <= step + 1 < len(units) and (step + 1) % 2 == 1 and units[step + 1][3] == SLICE:
                r, c, inside, width = units[step + 1]
                banks[step + 1] = regroup_on_tensor(
                    nc,
                    turn_psum,
                    identity_bf16,
                    raws[(r, c)][:, :, inside + width - PE_COLS : inside + width],
                )
            if 0 <= step < len(units):
                r, c, inside, width = units[step]
                if c == 0 and inside == 0:
                    w_codes = quantised.tile([P, PASSES, ranges[r][2]], U32, align_bytes=64)
                    w_scales = quantised.tile([P, PASSES, ranges[r][2]], U8, align_bytes=64)
                    codes[r] = (w_codes, w_scales)
                scalar_passes = (
                    0.5 * len(activating)
                    + len([pair for pair in finishing if pair[0] == 1])
                    + (0 <= step - X_STEP < PASSES)
                )
                vector_passes = len(combining) + len(
                    [pair for pair in finishing if pair[0] == 2]
                )
                net = scalar_passes - vector_passes
                if step in banks:
                    vector_cols = width - PE_COLS
                else:
                    base = BASE_COLS if step >= 7 else 232
                    vector_cols = COL_STEP * round(
                        (base + PASS_COLS * (net + net_before)) / COL_STEP
                    )
                net_before = net if step in banks else 0
                if width == PAIR:
                    vector_cols = PAIR_VECTOR_COLS
                regrouped[step] = regroup(
                    nc,
                    grouped_pool,
                    raws[(r, c)][:, :, inside : inside + width],
                    width,
                    vector_cols,
                    banks.get(step),
                )
                if inside + width == ranges[r][2]:
                    at = r * PASSES + c + RAW_BUFS
                    if at < len(loads):
                        load_pass(*loads[at])
            for pair in combining:
                combine(pair)
                to_turn.append((1, pair))
            if QUANTISE_LAG <= step < len(units) + QUANTISE_LAG:
                r, c, inside, width = units[step - QUANTISE_LAG]
                quantise_unit(regrouped[step - QUANTISE_LAG], r, c, inside, width)
                g, range_first, range_width = ranges[r]
                pairs = range((range_first + inside) // PAIR, (range_first + inside + width) // PAIR)
                if range_width == PAIR:
                    early_passes.extend([(g, pair, c) for pair in pairs])
                elif c == PASSES - 1:
                    waiting.extend([(g, pair, half) for pair in pairs for half in range(2)])
            for g, pair in finishing:
                finish(g, pair)
                finished += 1
            for g, pair, half in activating:
                activate(g, pair, half)
                if half == 1:
                    if g == 0:
                        finished += 1
                    elif g == 1:
                        to_combine.append(pair)
                    else:
                        to_turn.append((g, pair))
            step += 1
